import numpy as np
import ml_dtypes


def mxq(x, axis, fmt="e4m3"):
    dtype, down = {"e4m3": (ml_dtypes.float8_e4m3fn, 7), "e5m2": (ml_dtypes.float8_e5m2, 14)}[fmt]
    v = np.moveaxis(np.asarray(x, np.float32).astype(ml_dtypes.bfloat16).astype(np.float64), axis, -1)
    blocks = v.reshape(v.shape[:-1] + (-1, 32))
    amax = np.abs(blocks).max(-1, keepdims=True)
    byte = np.maximum(np.where(amax > 0, np.frexp(amax)[1] - 1 + 127, 0) - down, 1)
    scale = np.exp2(byte - 127.0)
    codes = (blocks / scale).astype(np.float32).astype(dtype).astype(np.float64)
    return np.moveaxis((codes * scale).reshape(v.shape), -1, axis)


WIDE = False


def mx_kscale(k):
    if not WIDE:
        return np.ones(k)
    levels = np.array([10, -10, 5, -5, 0])
    a = np.random.permutation(np.resize(levels, k // 512 * 4)).reshape(k // 512, 4)
    idx = np.arange(k)
    return np.exp2(a[idx // 512, idx % 128 // 32])


BF16 = ml_dtypes.bfloat16


def bf(x):
    return np.asarray(x, np.float32).astype(BF16)


def f64(x):
    return np.asarray(x).astype(np.float64)


B, N, D, C, H, NS = 2, 1024, 1024, 1024, 16, 10
HD = C // H
D4 = (0.4829629131445341, 0.8365163037378079, 0.2241438680420134, -0.1294095225512604)


def causal_multiscale(x_c, scale_gain):
    g = np.exp(scale_gain - scale_gain.max(0, keepdims=True))
    gains = g / g.sum(0, keepdims=True)
    gains_exp = np.repeat(gains, HD, axis=1)
    out = np.zeros_like(x_c)
    for j in range(NS):
        d = 2 ** j
        xp = np.pad(x_c, ((0, 0), (0, 0), (3 * d, 0)))
        y = (D4[0] * xp[:, :, 0 * d:0 * d + N]
             + D4[1] * xp[:, :, 1 * d:1 * d + N]
             + D4[2] * xp[:, :, 2 * d:2 * d + N]
             + D4[3] * xp[:, :, 3 * d:3 * d + N])
        out = out + gains_exp[j][None, :, None] * y
    return out


def setup_inputs():
    s = mx_kscale(D)
    return {"x": bf(np.random.standard_normal((B, N, D)) * s),
            "k_w": bf(np.random.standard_normal((C, D)) / np.sqrt(D) / s[None, :]),
            "k_b": bf(np.random.standard_normal(C) * 0.2),
            "v_w": bf(np.random.standard_normal((C, D)) / np.sqrt(D) / s[None, :]),
            "v_b": bf(np.random.standard_normal(C) * 0.2),
            "scale_gain": bf(np.random.standard_normal((NS, H)) * 0.5)}


def reference(x, k_w, k_b, v_w, v_b, scale_gain):
    xq = mxq(f64(x), 2, "e4m3")
    k = ((xq @ mxq(f64(k_w), 1, "e4m3").T) + f64(k_b)).reshape(B, N, H, HD)
    v = ((xq @ mxq(f64(v_w), 1, "e4m3").T) + f64(v_b)).reshape(B, N, H, HD)
    k_mag = np.sqrt((k * k).sum(-1, keepdims=True))
    field = v * k_mag
    x_c = field.transpose(0, 2, 3, 1).reshape(B, C, N)
    return causal_multiscale(x_c, f64(scale_gain))

@@ -1,0 +1,229 @@
+from contextlib import ExitStack
+
+import concourse.bass as bass
+import concourse.mybir as mybir
+import concourse.tile as tile
+from concourse.masks import make_identity
+
+F32 = mybir.dt.float32
+BF16 = mybir.dt.bfloat16
+U32 = mybir.dt.uint32
+U8 = mybir.dt.uint8
+FP8X4 = mybir.dt.float8_e4m3fn_x4
+ALU = mybir.AluOpType
+ACT = mybir.ActivationFunctionType
+AX = mybir.AxisListType
+
+P = 128
+B, N, D, C, H, NS = 2, 1024, 1024, 1024, 16, 10
+HD = C // H
+T0, T1, T2, T3 = (0.4829629131445341, 0.8365163037378079, 0.2241438680420134, -0.1294095225512604)
+ROW = 384
+FLOPS = 2 * (B * N) * D * (2 * C)
+
+
+def tile_causalwaveletfieldattentionbyte_pa_kernel(tc, x, k_w, k_b, v_w, v_b, scale_gain, out):
+    nc = tc.nc
+    with ExitStack() as ctx:
+        const = ctx.enter_context(tc.tile_pool(name="const", bufs=1))
+        rawp = ctx.enter_context(tc.tile_pool(name="rawp", bufs=4))
+        grpp = ctx.enter_context(tc.tile_pool(name="grpp", bufs=2))
+        work = ctx.enter_context(tc.tile_pool(name="work", bufs=3))
+        small = ctx.enter_context(tc.tile_pool(name="small", bufs=4))
+        accp = ctx.enter_context(tc.tile_pool(name="accp", bufs=3))
+        psum = ctx.enter_context(tc.psum_pool(name="psum", bufs=2))
+
+        ident = const.tile([P, P], F32)
+        make_identity(nc, ident[:])
+
+        sg_bf = const.tile([P, NS * H], BF16)
+        nc.scalar.dma_start(out=sg_bf[:], in_=scale_gain.rearrange("j h -> (j h)").partition_broadcast(P))
+        kbias = const.tile([P, C], BF16)
+        nc.scalar.dma_start(out=kbias[:], in_=k_b.partition_broadcast(P))
+        vbias = const.tile([P, C], BF16)
+        nc.scalar.dma_start(out=vbias[:], in_=v_b.partition_broadcast(P))
+
+        def load_x(b, s):
+            raw = rawp.tile([P, 4 * D], BF16, tag="raw")
+            nc.sync.dma_start(
+                out=raw[:].rearrange("p (r d) -> p r d", r=4),
+                in_=x[b, s * 512:(s + 1) * 512, :].rearrange("(a r) d -> a r d", r=4),
+            )
+            return raw
+
+        def load_w(w, hh):
+            raw = rawp.tile([P, 4 * D], BF16, tag="raw")
+            nc.sync.dma_start(
+                out=raw[:].rearrange("p (i d) -> p i d", i=4),
+                in_=w[hh * 512:(hh + 1) * 512, :].rearrange("(i p) d -> p i d", p=P),
+            )
+            return raw
+
+        g = const.tile([P, NS, H], F32)
+        nc.vector.tensor_copy(out=g[:], in_=sg_bf[:].rearrange("p (j h) -> p j h", j=NS))
+        gmax = const.tile([P, H], F32)
+        nc.vector.tensor_reduce(out=gmax[:], in_=g[:].rearrange("p j h -> p h j"), axis=AX.X, op=ALU.max)
+        nc.vector.tensor_tensor(out=g[:], in0=g[:], in1=gmax[:].unsqueeze(1).to_broadcast([P, NS, H]), op=ALU.subtract)
+        nc.scalar.activation(out=g[:], in_=g[:], func=ACT.Exp)
+        gsum = const.tile([P, H], F32)
+        nc.vector.tensor_reduce(out=gsum[:], in_=g[:].rearrange("p j h -> p h j"), axis=AX.X, op=ALU.add)
+        grec = const.tile([P, H], F32)
+        nc.vector.reciprocal(out=grec[:], in_=gsum[:])
+        nc.vector.tensor_tensor(out=g[:], in0=g[:], in1=grec[:].unsqueeze(1).to_broadcast([P, NS, H]), op=ALU.mult)
+        pow2 = const.tile([P, NS, H], F32)
+        nc.vector.tensor_scalar_mul(out=pow2[:], in0=g[:], scalar1=T2)
+        nc.vector.scalar_tensor_tensor(
+            out=pow2[:, 1:NS, :], in0=g[:, 0:NS - 1, :], scalar=T1, in1=pow2[:, 1:NS, :], op0=ALU.mult, op1=ALU.add
+        )
+        thr2 = const.tile([P, NS, H], F32)
+        nc.vector.tensor_scalar_mul(out=thr2[:], in0=g[:], scalar1=T0)
+
+        toep = const.tile([P, H * ROW], F32)
+        rows = toep[:].rearrange("p (h w) -> p h w", w=ROW)
+        nc.vector.memset(toep[:], 0.0)
+        gone = const.tile([P, H], F32)
+        nc.vector.tensor_reduce(out=gone[:], in_=g[:].rearrange("p j h -> p h j"), axis=AX.X, op=ALU.add)
+        nc.vector.tensor_scalar_mul(out=rows[:, :, 0:1], in0=gone[:].unsqueeze(2), scalar1=T3)
+        for j in range(2, NS):
+            kk = 2 ** (j - 2)
+            nc.vector.tensor_copy(out=rows[:, :, kk:kk + 1], in_=pow2[:, j, :].unsqueeze(2))
+        for j in range(2, NS - 1):
+            kk = 3 * 2 ** (j - 2)
+            nc.vector.tensor_copy(out=rows[:, :, kk:kk + 1], in_=thr2[:, j, :].unsqueeze(2))
+        period = H * ROW
+        flat = out[1].rearrange("c n -> (c n)")
+        nc.sync.dma_start(out=flat[0:P * period].rearrange("(a w) -> a w", w=period), in_=toep[:])
+        used = (H - 1) * ROW + 256
+        nc.sync.dma_start(
+            out=toep[:, 0:used],
+            in_=flat[0:P * (period - 1)].rearrange("(a w) -> a w", w=period - 1)[:, 0:used],
+        )
+
+        xq = const.tile([P, 2 * B * N], U32, align_bytes=64)
+        xs = const.tile([P, 2 * B * N], U8, align_bytes=64)
+        wq = const.tile([P, 2 * 2 * C], U32, align_bytes=64)
+        ws = const.tile([P, 2 * 2 * C], U8, align_bytes=64)
+        xq_v = xq[:].rearrange("p (g c) -> p g c", g=2)
+        xs_v = xs[:].rearrange("p (g c) -> p g c", g=2)
+        wq_v = wq[:].rearrange("p (g c) -> p g c", g=2)
+        ws_v = ws[:].rearrange("p (g c) -> p g c", g=2)
+
+        field = const.tile([P, 8 * H * 2 * HD], F32)
+        field_v = field[:].rearrange("p (q h b c) -> p q h b c", q=8, h=H, b=2)
+
+        flip = [0]
+
+        def quantise_chunk(raw, codes, scales, c0):
+            raw32 = raw[:].bitcast(F32)
+            grp = grpp.tile([P, 2 * 2048], BF16, tag="grp", align_bytes=64)
+            grp32 = grp[:].bitcast(F32).rearrange("p (g c u) -> p g c u", g=2, u=2)
+            for j in range(4):
+                pt = psum.tile([P, 4, P], F32, tag="f", bufs=4)
+                for gu in range(4):
+                    nc.tensor.transpose(pt[:, gu, :], raw32[:, j * 512 + gu * P:j * 512 + (gu + 1) * P], ident[:])
+                src = pt[:].rearrange("p (g u) c -> p g c u", u=2)
+                dst = grp32[:, :, j * P:(j + 1) * P, :]
+                if flip[0] % 4 != 3:
+                    nc.scalar.copy(out=dst, in_=src)
+                else:
+                    nc.vector.tensor_copy(out=dst, in_=src)
+                flip[0] += 1
+            for gg in range(2):
+                nc.vector.quantize_mx(
+                    out=codes[:, gg, c0:c0 + 512].bitcast(FP8X4),
+                    scales=scales[:, gg, c0:c0 + 512],
+                    in_=grp[:, gg * 2048:(gg + 1) * 2048],
+                )
+
+        def project(t, hh, tag):
+            b, q = t // 8, t % 8
+            ps_k = psum.tile([P, 512], F32, tag=tag)
+            ps_v = psum.tile([P, 512], F32, tag=tag)
+            for ps, base in ((ps_k, 0), (ps_v, C)):
+                w0 = base + hh * 512
+                for gg in range(2):
+                    nc.tensor.matmul_mx(
+                        out=ps[:],
+                        lhsT=xq_v[:, gg, t * P:(t + 1) * P].bitcast(FP8X4),
+                        lhsT_scale=xs_v[:, gg, t * P:(t + 1) * P],
+                        rhs=wq_v[:, gg, w0:w0 + 512].bitcast(FP8X4),
+                        rhs_scale=ws_v[:, gg, w0:w0 + 512],
+                        start=(gg == 0),
+                        stop=(gg == 1),
+                    )
+            kb = work.tile([P, 512], F32, tag="kb")
+            nc.vector.tensor_tensor(out=kb[:], in0=ps_k[:], in1=kbias[:, hh * 512:(hh + 1) * 512], op=ALU.add)
+            msq = small.tile([P, 8], F32, tag="msq")
+            for i in range(8):
+                nc.scalar.activation(
+                    out=kb[:, i * HD:(i + 1) * HD], in_=kb[:, i * HD:(i + 1) * HD], func=ACT.Square,
+                    accum_out=msq[:, i:i + 1],
+                )
+            mag = small.tile([P, 8], F32, tag="mag")
+            nc.scalar.activation(out=mag[:], in_=msq[:], func=ACT.Sqrt)
+            vb = work.tile([P, 512], F32, tag="vb")
+            nc.vector.tensor_tensor(out=vb[:], in0=ps_v[:], in1=vbias[:, hh * 512:(hh + 1) * 512], op=ALU.add)
+            nc.gpsimd.tensor_tensor(
+                out=field_v[:, q, hh * 8:(hh + 1) * 8, b, :],
+                in0=vb[:].rearrange("p (h c) -> p h c", c=HD),
+                in1=mag[:].unsqueeze(2).to_broadcast([P, 8, HD]),
+                op=ALU.mult,
+            )
+
+        def filter_head(h, tag):
+            f0 = psum.tile([P, 512], F32, tag="f", bufs=4)
+            f1 = psum.tile([P, 512], F32, tag="f", bufs=4)
+            o0 = psum.tile([P, 512], F32, tag=tag)
+            o1 = psum.tile([P, 512], F32, tag=tag)
+            o0v = o0[:].rearrange("p (a r) -> p a r", r=4)
+            o1v = o1[:].rearrange("p (a r) -> p a r", r=4)
+            f0v = f0[:].rearrange("p (a r) -> p a r", r=4)
+            f1v = f1[:].rearrange("p (a r) -> p a r", r=4)
+            near = toep[:, h * ROW:h * ROW + P]
+            far = toep[:, h * ROW + P:h * ROW + 2 * P]
+            st = [field_v[:, q, h, :, :].rearrange("p b c -> p (b c)") for q in range(8)]
+            for r in range(4):
+                nc.tensor.transpose(f0v[:, :, r], st[r], ident[:])
+            for r in range(4):
+                nc.tensor.transpose(f1v[:, :, r], st[4 + r], ident[:])
+            for r in range(4):
+                nc.tensor.matmul(o0v[:, :, r], lhsT=st[r], rhs=near, start=True, stop=True)
+            for r in range(4):
+                nc.tensor.matmul(o1v[:, :, r], lhsT=st[r], rhs=far, start=True, stop=False)
+                nc.tensor.matmul(o1v[:, :, r], lhsT=st[4 + r], rhs=near, start=False, stop=True)
+            acc = accp.tile([P, N], F32, tag="acc")
+            nc.scalar.copy(out=acc[:, 0:512], in_=o0[:])
+            nc.scalar.copy(out=acc[:, 512:N], in_=o1[:])
+            one = accp.tile([P, N], F32, tag="one")
+            nc.scalar.activation(out=one[:, 1:513], in_=f0[:], func=ACT.Copy, scale=pow2[:, 0, h:h + 1])
+            nc.scalar.activation(out=one[:, 513:N], in_=f1[:, 0:511], func=ACT.Copy, scale=pow2[:, 0, h:h + 1])
+            taps = ((2, pow2[:, 1, h:h + 1]), (3, thr2[:, 0, h:h + 1]), (6, thr2[:, 1, h:h + 1]))
+            for o, coef in taps:
+                nc.vector.scalar_tensor_tensor(
+                    out=acc[:, o:512 + o], in0=f0[:], scalar=coef, in1=acc[:, o:512 + o], op0=ALU.mult, op1=ALU.add
+                )
+                nc.vector.scalar_tensor_tensor(
+                    out=acc[:, 512 + o:N], in0=f1[:, 0:512 - o], scalar=coef, in1=acc[:, 512 + o:N],
+                    op0=ALU.mult, op1=ALU.add,
+                )
+            nc.gpsimd.tensor_tensor(out=acc[:, 1:N], in0=acc[:, 1:N], in1=one[:, 1:N], op=ALU.add)
+            nc.sync.dma_start(out=out[0, h * HD:(h + 1) * HD, :], in_=acc[0:HD, :])
+            nc.sync.dma_start(out=out[1, h * HD:(h + 1) * HD, :], in_=acc[HD:P, :])
+
+        quantise_chunk(load_x(0, 0), xq_v, xs_v, 0)
+        quantise_chunk(load_w(k_w, 0), wq_v, ws_v, 0)
+        quantise_chunk(load_w(v_w, 0), wq_v, ws_v, C)
+        for t in range(0, 4):
+            project(t, 0, ("mx", "o")[t % 2])
+        for ch in range(1, 4):
+            quantise_chunk(load_x(ch // 2, ch % 2), xq_v, xs_v, ch * 512)
+            for t in range(4 * ch, 4 * ch + 4):
+                project(t, 0, ("mx", "o")[t % 2])
+        quantise_chunk(load_w(k_w, 1), wq_v, ws_v, 512)
+        quantise_chunk(load_w(v_w, 1), wq_v, ws_v, C + 512)
+        for i in range(8):
+            project(2 * i, 1, "mx")
+            project(2 * i + 1, 1, "mx")
+            filter_head(i, "o")
+        for h in range(8, H):
+            filter_head(h, ("o", "mx")[h % 2])

@@ -175,40 +175,46 @@ def tile_causalwaveletfieldattentionbyte_pa_kernel(tc, x, k_w, k_b, v_w, v_b, sc
             f1 = psum.tile([P, 512], F32, tag="f", bufs=4)
             o0 = psum.tile([P, 512], F32, tag=tag)
             o1 = psum.tile([P, 512], F32, tag=tag)
-            o0v = o0[:].rearrange("p (a r) -> p a r", r=4)
-            o1v = o1[:].rearrange("p (a r) -> p a r", r=4)
-            f0v = f0[:].rearrange("p (a r) -> p a r", r=4)
-            f1v = f1[:].rearrange("p (a r) -> p a r", r=4)
+            o0n = o0[:].rearrange("p (r a) -> p a r", r=4)
+            o1n = o1[:].rearrange("p (r a) -> p a r", r=4)
+            f0n = f0[:].rearrange("p (r a) -> p a r", r=4)
+            f1n = f1[:].rearrange("p (r a) -> p a r", r=4)
+
+            def tok(ap):
+                return ap.rearrange("p (a r) -> p a r", r=4)
+
             near = toep[:, h * ROW:h * ROW + P]
             far = toep[:, h * ROW + P:h * ROW + 2 * P]
             st = [field_v[:, q, h, :, :].rearrange("p b c -> p (b c)") for q in range(8)]
             for r in range(4):
-                nc.tensor.transpose(f0v[:, :, r], st[r], ident[:])
+                nc.tensor.transpose(f0[:, r * P:(r + 1) * P], st[r], ident[:])
             for r in range(4):
-                nc.tensor.transpose(f1v[:, :, r], st[4 + r], ident[:])
+                nc.tensor.transpose(f1[:, r * P:(r + 1) * P], st[4 + r], ident[:])
             for r in range(4):
-                nc.tensor.matmul(o0v[:, :, r], lhsT=st[r], rhs=near, start=True, stop=True)
+                nc.tensor.matmul(o0[:, r * P:(r + 1) * P], lhsT=st[r], rhs=near, start=True, stop=True)
             for r in range(4):
-                nc.tensor.matmul(o1v[:, :, r], lhsT=st[r], rhs=far, start=True, stop=False)
-                nc.tensor.matmul(o1v[:, :, r], lhsT=st[4 + r], rhs=near, start=False, stop=True)
-            acc = accp.tile([P, N], F32, tag="acc")
-            nc.scalar.copy(out=acc[:, 0:512], in_=o0[:])
-            nc.scalar.copy(out=acc[:, 512:N], in_=o1[:])
-            one = accp.tile([P, N], F32, tag="one")
-            nc.scalar.activation(out=one[:, 1:513], in_=f0[:], func=ACT.Copy, scale=pow2[:, 0, h:h + 1])
-            nc.scalar.activation(out=one[:, 513:N], in_=f1[:, 0:511], func=ACT.Copy, scale=pow2[:, 0, h:h + 1])
+                nc.tensor.matmul(o1[:, r * P:(r + 1) * P], lhsT=st[r], rhs=far, start=True, stop=False)
+                nc.tensor.matmul(o1[:, r * P:(r + 1) * P], lhsT=st[4 + r], rhs=near, start=False, stop=True)
+            acc = accp.tile([P, N + 8], F32, tag="acc")
+            nc.gpsimd.memset(acc[:, N:N + 8], 0.0)
+            nc.scalar.copy(out=tok(acc[:, 0:512]), in_=o0n)
+            nc.scalar.copy(out=tok(acc[:, 512:N]), in_=o1n)
+            one = accp.tile([P, N + 8], F32, tag="one")
+            nc.scalar.activation(out=tok(one[:, 1:513]), in_=f0n, func=ACT.Copy, scale=pow2[:, 0, h:h + 1])
+            nc.scalar.activation(out=tok(one[:, 513:N + 1]), in_=f1n, func=ACT.Copy, scale=pow2[:, 0, h:h + 1])
             taps = ((2, pow2[:, 1, h:h + 1]), (3, thr2[:, 0, h:h + 1]), (6, thr2[:, 1, h:h + 1]))
             for o, coef in taps:
                 nc.vector.scalar_tensor_tensor(
-                    out=acc[:, o:512 + o], in0=f0[:], scalar=coef, in1=acc[:, o:512 + o], op0=ALU.mult, op1=ALU.add
+                    out=tok(acc[:, o:512 + o]), in0=f0n, scalar=coef, in1=tok(acc[:, o:512 + o]),
+                    op0=ALU.mult, op1=ALU.add,
                 )
                 nc.vector.scalar_tensor_tensor(
-                    out=acc[:, 512 + o:N], in0=f1[:, 0:512 - o], scalar=coef, in1=acc[:, 512 + o:N],
+                    out=tok(acc[:, 512 + o:N + o]), in0=f1n, scalar=coef, in1=tok(acc[:, 512 + o:N + o]),
                     op0=ALU.mult, op1=ALU.add,
                 )
             nc.gpsimd.tensor_tensor(out=acc[:, 1:N], in0=acc[:, 1:N], in1=one[:, 1:N], op=ALU.add)
-            nc.sync.dma_start(out=out[0, h * HD:(h + 1) * HD, :], in_=acc[0:HD, :])
-            nc.sync.dma_start(out=out[1, h * HD:(h + 1) * HD, :], in_=acc[HD:P, :])
+            nc.sync.dma_start(out=out[0, h * HD:(h + 1) * HD, :], in_=acc[0:HD, 0:N])
+            nc.sync.dma_start(out=out[1, h * HD:(h + 1) * HD, :], in_=acc[HD:P, 0:N])
 
         quantise_chunk(load_x(0, 0), xq_v, xs_v, 0)
         quantise_chunk(load_w(k_w, 0), wq_v, ws_v, 0)

@@ -31,10 +31,14 @@ def tile_causalwaveletfieldattentionbyte_pa_kernel(tc, x, k_w, k_b, v_w, v_b, sc
         work = ctx.enter_context(tc.tile_pool(name="work", bufs=3))
         small = ctx.enter_context(tc.tile_pool(name="small", bufs=4))
         accp = ctx.enter_context(tc.tile_pool(name="accp", bufs=3))
-        psum = ctx.enter_context(tc.psum_pool(name="psum", bufs=2))
+        psum = ctx.enter_context(tc.psum_pool(name="psum", bufs=1))
+        ctx.enter_context(tc.manual_schedule())
 
         ident = const.tile([P, P], F32)
         make_identity(nc, ident[:])
+
+        def bank(i):
+            return psum.tile([P, 512], F32, tag="b%d" % i, name="bank%d" % i)
 
         sg_bf = const.tile([P, NS * H], BF16)
         nc.scalar.dma_start(out=sg_bf[:], in_=scale_gain.rearrange("j h -> (j h)").partition_broadcast(P))
@@ -60,44 +64,50 @@ def tile_causalwaveletfieldattentionbyte_pa_kernel(tc, x, k_w, k_b, v_w, v_b, sc
             return raw
 
         g = const.tile([P, NS, H], F32)
-        nc.vector.tensor_copy(out=g[:], in_=sg_bf[:].rearrange("p (j h) -> p j h", j=NS))
         gmax = const.tile([P, H], F32)
-        nc.vector.tensor_reduce(out=gmax[:], in_=g[:].rearrange("p j h -> p h j"), axis=AX.X, op=ALU.max)
-        nc.vector.tensor_tensor(out=g[:], in0=g[:], in1=gmax[:].unsqueeze(1).to_broadcast([P, NS, H]), op=ALU.subtract)
-        nc.scalar.activation(out=g[:], in_=g[:], func=ACT.Exp)
         gsum = const.tile([P, H], F32)
-        nc.vector.tensor_reduce(out=gsum[:], in_=g[:].rearrange("p j h -> p h j"), axis=AX.X, op=ALU.add)
         grec = const.tile([P, H], F32)
-        nc.vector.reciprocal(out=grec[:], in_=gsum[:])
-        nc.vector.tensor_tensor(out=g[:], in0=g[:], in1=grec[:].unsqueeze(1).to_broadcast([P, NS, H]), op=ALU.mult)
+        gone = const.tile([P, H], F32)
         pow2 = const.tile([P, NS, H], F32)
-        nc.vector.tensor_scalar_mul(out=pow2[:], in0=g[:], scalar1=T2)
-        nc.vector.scalar_tensor_tensor(
-            out=pow2[:, 1:NS, :], in0=g[:, 0:NS - 1, :], scalar=T1, in1=pow2[:, 1:NS, :], op0=ALU.mult, op1=ALU.add
-        )
         thr2 = const.tile([P, NS, H], F32)
-        nc.vector.tensor_scalar_mul(out=thr2[:], in0=g[:], scalar1=T0)
-
         toep = const.tile([P, H * ROW], F32)
         rows = toep[:].rearrange("p (h w) -> p h w", w=ROW)
-        nc.vector.memset(toep[:], 0.0)
-        gone = const.tile([P, H], F32)
-        nc.vector.tensor_reduce(out=gone[:], in_=g[:].rearrange("p j h -> p h j"), axis=AX.X, op=ALU.add)
-        nc.vector.tensor_scalar_mul(out=rows[:, :, 0:1], in0=gone[:].unsqueeze(2), scalar1=T3)
-        for j in range(2, NS):
-            kk = 2 ** (j - 2)
-            nc.vector.tensor_copy(out=rows[:, :, kk:kk + 1], in_=pow2[:, j, :].unsqueeze(2))
-        for j in range(2, NS - 1):
-            kk = 3 * 2 ** (j - 2)
-            nc.vector.tensor_copy(out=rows[:, :, kk:kk + 1], in_=thr2[:, j, :].unsqueeze(2))
         period = H * ROW
-        flat = out[1].rearrange("c n -> (c n)")
-        nc.sync.dma_start(out=flat[0:P * period].rearrange("(a w) -> a w", w=period), in_=toep[:])
         used = (H - 1) * ROW + 256
-        nc.sync.dma_start(
-            out=toep[:, 0:used],
-            in_=flat[0:P * (period - 1)].rearrange("(a w) -> a w", w=period - 1)[:, 0:used],
-        )
+        flat = out[1].rearrange("c n -> (c n)")
+
+        def gains():
+            by_head = g[:].rearrange("p j h -> p h j")
+            nc.vector.memset(toep[:], 0.0)
+            nc.vector.tensor_copy(out=g[:], in_=sg_bf[:].rearrange("p (j h) -> p j h", j=NS))
+            nc.vector.tensor_reduce(out=gmax[:], in_=by_head, axis=AX.X, op=ALU.max)
+            nc.vector.tensor_tensor(out=g[:], in0=g[:], in1=gmax[:].unsqueeze(1).to_broadcast([P, NS, H]), op=ALU.subtract)
+            nc.scalar.activation(out=g[:], in_=g[:], func=ACT.Exp)
+            nc.vector.tensor_reduce(out=gsum[:], in_=by_head, axis=AX.X, op=ALU.add)
+            nc.vector.reciprocal(out=grec[:], in_=gsum[:])
+            nc.vector.tensor_tensor(out=g[:], in0=g[:], in1=grec[:].unsqueeze(1).to_broadcast([P, NS, H]), op=ALU.mult)
+            nc.vector.tensor_scalar_mul(out=pow2[:], in0=g[:], scalar1=T2)
+            nc.vector.scalar_tensor_tensor(
+                out=pow2[:, 1:NS, :], in0=g[:, 0:NS - 1, :], scalar=T1, in1=pow2[:, 1:NS, :], op0=ALU.mult, op1=ALU.add
+            )
+            nc.vector.tensor_scalar_mul(out=thr2[:], in0=g[:], scalar1=T0)
+            nc.vector.tensor_reduce(out=gone[:], in_=by_head, axis=AX.X, op=ALU.add)
+            nc.vector.tensor_scalar_mul(out=rows[:, :, 0:1], in0=gone[:].unsqueeze(2), scalar1=T3)
+            for j in range(2, NS):
+                kk = 2 ** (j - 2)
+                nc.vector.tensor_copy(out=rows[:, :, kk:kk + 1], in_=pow2[:, j, :].unsqueeze(2))
+            for j in range(2, NS - 1):
+                kk = 3 * 2 ** (j - 2)
+                nc.vector.tensor_copy(out=rows[:, :, kk:kk + 1], in_=thr2[:, j, :].unsqueeze(2))
+
+        def toeplitz_out():
+            nc.sync.dma_start(out=flat[0:P * period].rearrange("(a w) -> a w", w=period), in_=toep[:])
+
+        def toeplitz_back():
+            nc.sync.dma_start(
+                out=toep[:, 0:used],
+                in_=flat[0:P * (period - 1)].rearrange("(a w) -> a w", w=period - 1)[:, 0:used],
+            )
 
         xq = const.tile([P, 2 * B * N], U32, align_bytes=64)
         xs = const.tile([P, 2 * B * N], U8, align_bytes=64)
@@ -111,23 +121,29 @@ def tile_causalwaveletfieldattentionbyte_pa_kernel(tc, x, k_w, k_b, v_w, v_b, sc
         field = const.tile([P, 8 * H * 2 * HD], F32)
         field_v = field[:].rearrange("p (q h b c) -> p q h b c", q=8, h=H, b=2)
 
-        flip = [0]
-
-        def quantise_chunk(raw, codes, scales, c0):
+        def flip_pe(raw):
             raw32 = raw[:].bitcast(F32)
+            pts = []
+            for j in range(4):
+                pt = bank(j)
+                for gu in range(4):
+                    nc.tensor.transpose(pt[:, gu * P:(gu + 1) * P], raw32[:, j * 512 + gu * P:j * 512 + (gu + 1) * P], ident[:])
+                pts.append(pt)
+            return pts
+
+        def flip_out(pts, engines):
             grp = grpp.tile([P, 2 * 2048], BF16, tag="grp", align_bytes=64)
             grp32 = grp[:].bitcast(F32).rearrange("p (g c u) -> p g c u", g=2, u=2)
             for j in range(4):
-                pt = psum.tile([P, 4, P], F32, tag="f", bufs=4)
-                for gu in range(4):
-                    nc.tensor.transpose(pt[:, gu, :], raw32[:, j * 512 + gu * P:j * 512 + (gu + 1) * P], ident[:])
-                src = pt[:].rearrange("p (g u) c -> p g c u", u=2)
+                src = pts[j][:].rearrange("p (g u c) -> p g c u", g=2, u=2)
                 dst = grp32[:, :, j * P:(j + 1) * P, :]
-                if flip[0] % 4 != 3:
+                if engines[j] == "s":
                     nc.scalar.copy(out=dst, in_=src)
                 else:
                     nc.vector.tensor_copy(out=dst, in_=src)
-                flip[0] += 1
+            return grp
+
+        def quantise(grp, codes, scales, c0):
             for gg in range(2):
                 nc.vector.quantize_mx(
                     out=codes[:, gg, c0:c0 + 512].bitcast(FP8X4),
@@ -135,11 +151,9 @@ def tile_causalwaveletfieldattentionbyte_pa_kernel(tc, x, k_w, k_b, v_w, v_b, sc
                     in_=grp[:, gg * 2048:(gg + 1) * 2048],
                 )
 
-        def project(t, hh, tag):
-            b, q = t // 8, t % 8
-            ps_k = psum.tile([P, 512], F32, tag=tag)
-            ps_v = psum.tile([P, 512], F32, tag=tag)
-            for ps, base in ((ps_k, 0), (ps_v, C)):
+        def proj_pe(t, hh, b0):
+            pair = (bank(b0), bank(b0 + 1))
+            for ps, base in zip(pair, (0, C)):
                 w0 = base + hh * 512
                 for gg in range(2):
                     nc.tensor.matmul_mx(
@@ -151,8 +165,16 @@ def tile_causalwaveletfieldattentionbyte_pa_kernel(tc, x, k_w, k_b, v_w, v_b, sc
                         start=(gg == 0),
                         stop=(gg == 1),
                     )
+            return pair
+
+        def proj_v(pair, hh):
             kb = work.tile([P, 512], F32, tag="kb")
-            nc.vector.tensor_tensor(out=kb[:], in0=ps_k[:], in1=kbias[:, hh * 512:(hh + 1) * 512], op=ALU.add)
+            nc.vector.tensor_tensor(out=kb[:], in0=pair[0][:], in1=kbias[:, hh * 512:(hh + 1) * 512], op=ALU.add)
+            vb = work.tile([P, 512], F32, tag="vb")
+            nc.vector.tensor_tensor(out=vb[:], in0=pair[1][:], in1=vbias[:, hh * 512:(hh + 1) * 512], op=ALU.add)
+            return kb, vb
+
+        def proj_s(kb):
             msq = small.tile([P, 8], F32, tag="msq")
             for i in range(8):
                 nc.scalar.activation(
@@ -161,75 +183,162 @@ def tile_causalwaveletfieldattentionbyte_pa_kernel(tc, x, k_w, k_b, v_w, v_b, sc
                 )
             mag = small.tile([P, 8], F32, tag="mag")
             nc.scalar.activation(out=mag[:], in_=msq[:], func=ACT.Sqrt)
-            vb = work.tile([P, 512], F32, tag="vb")
-            nc.vector.tensor_tensor(out=vb[:], in0=ps_v[:], in1=vbias[:, hh * 512:(hh + 1) * 512], op=ALU.add)
+            return mag
+
+        def proj_g(t, hh, vb, mag):
             nc.gpsimd.tensor_tensor(
-                out=field_v[:, q, hh * 8:(hh + 1) * 8, b, :],
+                out=field_v[:, t % 8, hh * 8:(hh + 1) * 8, t // 8, :],
                 in0=vb[:].rearrange("p (h c) -> p h c", c=HD),
                 in1=mag[:].unsqueeze(2).to_broadcast([P, 8, HD]),
                 op=ALU.mult,
             )
 
-        def filter_head(h, tag):
-            f0 = psum.tile([P, 512], F32, tag="f", bufs=4)
-            f1 = psum.tile([P, 512], F32, tag="f", bufs=4)
-            o0 = psum.tile([P, 512], F32, tag=tag)
-            o1 = psum.tile([P, 512], F32, tag=tag)
-            o0n = o0[:].rearrange("p (r a) -> p a r", r=4)
-            o1n = o1[:].rearrange("p (r a) -> p a r", r=4)
-            f0n = f0[:].rearrange("p (r a) -> p a r", r=4)
-            f1n = f1[:].rearrange("p (r a) -> p a r", r=4)
+        def tok(ap):
+            return ap.rearrange("p (a r) -> p a r", r=4)
 
-            def tok(ap):
-                return ap.rearrange("p (a r) -> p a r", r=4)
+        def planes(ap):
+            return ap.rearrange("p (r a) -> p a r", r=4)
 
-            near = toep[:, h * ROW:h * ROW + P]
-            far = toep[:, h * ROW + P:h * ROW + 2 * P]
-            st = [field_v[:, q, h, :, :].rearrange("p b c -> p (b c)") for q in range(8)]
+        def stat(h, q):
+            return field_v[:, q, h, :, :].rearrange("p b c -> p (b c)")
+
+        def filt_t(h, b0):
+            f0, f1 = bank(b0), bank(b0 + 1)
             for r in range(4):
-                nc.tensor.transpose(f0[:, r * P:(r + 1) * P], st[r], ident[:])
+                nc.tensor.transpose(f0[:, r * P:(r + 1) * P], stat(h, r), ident[:])
             for r in range(4):
-                nc.tensor.transpose(f1[:, r * P:(r + 1) * P], st[4 + r], ident[:])
+                nc.tensor.transpose(f1[:, r * P:(r + 1) * P], stat(h, 4 + r), ident[:])
+            return f0, f1
+
+        def filt_m0(h, b0):
+            o0 = bank(b0)
             for r in range(4):
-                nc.tensor.matmul(o0[:, r * P:(r + 1) * P], lhsT=st[r], rhs=near, start=True, stop=True)
-            for r in range(4):
-                nc.tensor.matmul(o1[:, r * P:(r + 1) * P], lhsT=st[r], rhs=far, start=True, stop=False)
-                nc.tensor.matmul(o1[:, r * P:(r + 1) * P], lhsT=st[4 + r], rhs=near, start=False, stop=True)
+                nc.tensor.matmul(o0[:, r * P:(r + 1) * P], lhsT=stat(h, r), rhs=toep[:, h * ROW:h * ROW + P], start=True, stop=True)
+            return o0
+
+        def filt_m1(h, o1, rs):
+            for r in rs:
+                nc.tensor.matmul(o1[:, r * P:(r + 1) * P], lhsT=stat(h, r), rhs=toep[:, h * ROW + P:h * ROW + 2 * P], start=True, stop=False)
+                nc.tensor.matmul(o1[:, r * P:(r + 1) * P], lhsT=stat(h, 4 + r), rhs=toep[:, h * ROW:h * ROW + P], start=False, stop=True)
+
+        def filt_one(h, f0, f1):
+            one = accp.tile([P, N + 8], F32, tag="one")
+            nc.scalar.activation(out=tok(one[:, 1:513]), in_=planes(f0[:]), func=ACT.Copy, scale=pow2[:, 0, h:h + 1])
+            nc.scalar.activation(out=tok(one[:, 513:N + 1]), in_=planes(f1[:]), func=ACT.Copy, scale=pow2[:, 0, h:h + 1])
+            return one
+
+        def filt_acc():
             acc = accp.tile([P, N + 8], F32, tag="acc")
             nc.gpsimd.memset(acc[:, N:N + 8], 0.0)
-            nc.scalar.copy(out=tok(acc[:, 0:512]), in_=o0n)
-            nc.scalar.copy(out=tok(acc[:, 512:N]), in_=o1n)
-            one = accp.tile([P, N + 8], F32, tag="one")
-            nc.scalar.activation(out=tok(one[:, 1:513]), in_=f0n, func=ACT.Copy, scale=pow2[:, 0, h:h + 1])
-            nc.scalar.activation(out=tok(one[:, 513:N + 1]), in_=f1n, func=ACT.Copy, scale=pow2[:, 0, h:h + 1])
-            taps = ((2, pow2[:, 1, h:h + 1]), (3, thr2[:, 0, h:h + 1]), (6, thr2[:, 1, h:h + 1]))
-            for o, coef in taps:
-                nc.vector.scalar_tensor_tensor(
-                    out=tok(acc[:, o:512 + o]), in0=f0n, scalar=coef, in1=tok(acc[:, o:512 + o]),
-                    op0=ALU.mult, op1=ALU.add,
-                )
-                nc.vector.scalar_tensor_tensor(
-                    out=tok(acc[:, 512 + o:N + o]), in0=f1n, scalar=coef, in1=tok(acc[:, 512 + o:N + o]),
-                    op0=ALU.mult, op1=ALU.add,
-                )
+            return acc
+
+        def tap(h, acc, f, half, which):
+            o, coef = ((2, pow2[:, 1, h:h + 1]), (3, thr2[:, 0, h:h + 1]), (6, thr2[:, 1, h:h + 1]))[which]
+            lo = half * 512 + o
+            nc.vector.scalar_tensor_tensor(
+                out=tok(acc[:, lo:lo + 512]), in0=planes(f[:]), scalar=coef, in1=tok(acc[:, lo:lo + 512]),
+                op0=ALU.mult, op1=ALU.add,
+            )
+
+        def filt_end(h, acc, one):
             nc.gpsimd.tensor_tensor(out=acc[:, 1:N], in0=acc[:, 1:N], in1=one[:, 1:N], op=ALU.add)
             nc.sync.dma_start(out=out[0, h * HD:(h + 1) * HD, :], in_=acc[0:HD, 0:N])
             nc.sync.dma_start(out=out[1, h * HD:(h + 1) * HD, :], in_=acc[HD:P, 0:N])
 
-        quantise_chunk(load_x(0, 0), xq_v, xs_v, 0)
-        quantise_chunk(load_w(k_w, 0), wq_v, ws_v, 0)
-        quantise_chunk(load_w(v_w, 0), wq_v, ws_v, C)
-        for t in range(0, 4):
-            project(t, 0, ("mx", "o")[t % 2])
-        for ch in range(1, 4):
-            quantise_chunk(load_x(ch // 2, ch % 2), xq_v, xs_v, ch * 512)
-            for t in range(4 * ch, 4 * ch + 4):
-                project(t, 0, ("mx", "o")[t % 2])
-        quantise_chunk(load_w(k_w, 1), wq_v, ws_v, 512)
-        quantise_chunk(load_w(v_w, 1), wq_v, ws_v, C + 512)
+        raws = [load_x(0, 0), load_w(k_w, 0), load_w(v_w, 0), load_x(0, 1)]
+        gains()
+        spots = ((xq_v, xs_v, 0), (wq_v, ws_v, 0), (wq_v, ws_v, C), (xq_v, xs_v, 512), (xq_v, xs_v, 1024),
+                 (xq_v, xs_v, 1536), (wq_v, ws_v, 512), (wq_v, ws_v, C + 512))
+        later = (lambda: load_x(1, 0), lambda: load_x(1, 1), lambda: load_w(k_w, 1), lambda: load_w(v_w, 1))
+        grps = []
+
+        def chunk(c, engines):
+            pts = flip_pe(raws[c])
+            if c < 4:
+                raws.append(later[c]())
+            if c == 3:
+                toeplitz_out()
+                toeplitz_back()
+            grps.append(flip_out(pts, engines))
+
+        def quant(c):
+            quantise(grps[c], spots[c][0], spots[c][1], spots[c][2])
+
+        def unit_tail(t, hh, pair):
+            kb, vb = proj_v(pair, hh)
+            mag = proj_s(kb)
+            proj_g(t, hh, vb, mag)
+
+        chunk(0, "svsv")
+        chunk(1, "svsv")
+        quant(0)
+        chunk(2, "svsv")
+        quant(1)
+        chunk(3, "svsv")
+        quant(2)
+        for c in range(4):
+            pend = []
+            for t in range(4 * c, 4 * c + 4):
+                pend.append((t, proj_pe(t, 0, 4 + 2 * (t % 2))))
+                if len(pend) == 2:
+                    unit_tail(pend[0][0], 0, pend[0][1])
+                    pend = pend[1:]
+                if t == 4 * c + 1:
+                    quant(c + 3)
+            chunk(c + 4, "svsv")
+            unit_tail(pend[0][0], 0, pend[0][1])
+        quant(7)
+
+        state = {}
+
+        def head_front(h, fb, ob):
+            f0, f1 = filt_t(h, fb)
+            o0 = filt_m0(h, ob)
+            o1 = bank(ob + 1)
+            state[h] = [f0, f1, o0, o1, None, None]
+
+        def head_scalar0(h):
+            f0, f1, o0, o1 = state[h][0:4]
+            acc = filt_acc()
+            state[h][4] = acc
+            state[h][5] = filt_one(h, f0, f1)
+            nc.scalar.copy(out=tok(acc[:, 0:512]), in_=planes(o0[:]))
+
+        def head_scalar1(h):
+            nc.scalar.copy(out=tok(state[h][4][:, 512:N]), in_=planes(state[h][3][:]))
+
+        def head_taps(h, part):
+            f0, f1, o0, o1, acc, one = state[h]
+            for which, half in (((0, 0), (0, 1), (1, 0)), ((1, 1), (2, 0), (2, 1)))[part]:
+                tap(h, acc, (f0, f1)[half], half, which)
+
         for i in range(8):
-            project(2 * i, 1, "mx")
-            project(2 * i + 1, 1, "mx")
-            filter_head(i, "o")
+            head_front(i, 2 * (i % 2), 4)
+            pa = proj_pe(2 * i, 1, 6)
+            if i > 0:
+                head_taps(i - 1, 0)
+            kb, vb = proj_v(pa, 1)
+            head_scalar0(i)
+            mag = proj_s(kb)
+            proj_g(2 * i, 1, vb, mag)
+            filt_m1(i, state[i][3], (0, 1))
+            pb = proj_pe(2 * i + 1, 1, 6)
+            if i > 0:
+                head_taps(i - 1, 1)
+                filt_end(i - 1, state[i - 1][4], state[i - 1][5])
+            kb, vb = proj_v(pb, 1)
+            filt_m1(i, state[i][3], (2, 3))
+            head_scalar1(i)
+            mag = proj_s(kb)
+            proj_g(2 * i + 1, 1, vb, mag)
         for h in range(8, H):
-            filter_head(h, ("o", "mx")[h % 2])
+            head_front(h, 2 * (h % 2), 4 + 2 * (h % 2))
+            head_taps(h - 1, 0)
+            head_scalar0(h)
+            filt_m1(h, state[h][3], (0, 1, 2, 3))
+            head_taps(h - 1, 1)
+            filt_end(h - 1, state[h - 1][4], state[h - 1][5])
+            head_scalar1(h)
+        head_taps(H - 1, 0)
+        head_taps(H - 1, 1)
+        filt_end(H - 1, state[H - 1][4], state[H - 1][5])

@@ -1,8 +1,6 @@
 from contextlib import ExitStack
 
-import concourse.bass as bass
 import concourse.mybir as mybir
-import concourse.tile as tile
 from concourse.masks import make_identity
 
 F32 = mybir.dt.float32
@@ -18,7 +16,10 @@ P = 128
 B, N, D, C, H, NS = 2, 1024, 1024, 1024, 16, 10
 HD = C // H
 T0, T1, T2, T3 = (0.4829629131445341, 0.8365163037378079, 0.2241438680420134, -0.1294095225512604)
-ROW = 384
+ROW = 320
+GROUP = 4 * ROW
+HALF = N // 2
+PAD = 8
 FLOPS = 2 * (B * N) * D * (2 * C)
 
 
@@ -28,17 +29,17 @@ def tile_causalwaveletfieldattentionbyte_pa_kernel(tc, x, k_w, k_b, v_w, v_b, sc
         const = ctx.enter_context(tc.tile_pool(name="const", bufs=1))
         rawp = ctx.enter_context(tc.tile_pool(name="rawp", bufs=4))
         grpp = ctx.enter_context(tc.tile_pool(name="grpp", bufs=2))
-        work = ctx.enter_context(tc.tile_pool(name="work", bufs=3))
-        small = ctx.enter_context(tc.tile_pool(name="small", bufs=4))
+        work = ctx.enter_context(tc.tile_pool(name="work", bufs=4))
+        small = ctx.enter_context(tc.tile_pool(name="small", bufs=6))
         accp = ctx.enter_context(tc.tile_pool(name="accp", bufs=3))
         psum = ctx.enter_context(tc.psum_pool(name="psum", bufs=1))
         ctx.enter_context(tc.manual_schedule())
 
-        ident = const.tile([P, P], F32)
-        make_identity(nc, ident[:])
-
         def bank(i):
             return psum.tile([P, 512], F32, tag="b%d" % i, name="bank%d" % i)
+
+        ident = const.tile([P, P], F32)
+        make_identity(nc, ident[:])
 
         sg_bf = const.tile([P, NS * H], BF16)
         nc.scalar.dma_start(out=sg_bf[:], in_=scale_gain.rearrange("j h -> (j h)").partition_broadcast(P))
@@ -46,21 +47,22 @@ def tile_causalwaveletfieldattentionbyte_pa_kernel(tc, x, k_w, k_b, v_w, v_b, sc
         nc.scalar.dma_start(out=kbias[:], in_=k_b.partition_broadcast(P))
         vbias = const.tile([P, C], BF16)
         nc.scalar.dma_start(out=vbias[:], in_=v_b.partition_broadcast(P))
+        kvb = const.tile([P, 2 * C], BF16)
+        kvb_v = kvb[:].rearrange("p (r m c) -> p r m c", m=2, c=P)
 
-        def load_x(b, s):
-            raw = rawp.tile([P, 4 * D], BF16, tag="raw")
+        def load_x(ch):
+            raw = rawp.tile([P, 4 * D], BF16, tag="rawx", bufs=3)
             nc.sync.dma_start(
                 out=raw[:].rearrange("p (r d) -> p r d", r=4),
-                in_=x[b, s * 512:(s + 1) * 512, :].rearrange("(a r) d -> a r d", r=4),
+                in_=x[ch // 2, (ch % 2) * HALF:(ch % 2 + 1) * HALF, :].rearrange("(a r) d -> a r d", r=4),
             )
             return raw
 
-        def load_w(w, hh):
-            raw = rawp.tile([P, 4 * D], BF16, tag="raw")
-            nc.sync.dma_start(
-                out=raw[:].rearrange("p (i d) -> p i d", i=4),
-                in_=w[hh * 512:(hh + 1) * 512, :].rearrange("(i p) d -> p i d", p=P),
-            )
+        def load_w(ch):
+            raw = rawp.tile([P, 4 * D], BF16, tag="raww", bufs=2)
+            view = raw[:].rearrange("p (i d) -> p i d", i=4)
+            nc.sync.dma_start(out=view[:, 0:2, :], in_=k_w[ch * 256:(ch + 1) * 256, :].rearrange("(i p) d -> p i d", p=P))
+            nc.sync.dma_start(out=view[:, 2:4, :], in_=v_w[ch * 256:(ch + 1) * 256, :].rearrange("(i p) d -> p i d", p=P))
             return raw
 
         g = const.tile([P, NS, H], F32)
@@ -72,8 +74,6 @@ def tile_causalwaveletfieldattentionbyte_pa_kernel(tc, x, k_w, k_b, v_w, v_b, sc
         thr2 = const.tile([P, NS, H], F32)
         toep = const.tile([P, H * ROW], F32)
         rows = toep[:].rearrange("p (h w) -> p h w", w=ROW)
-        period = H * ROW
-        used = (H - 1) * ROW + 256
         flat = out[1].rearrange("c n -> (c n)")
 
         def gains():
@@ -99,14 +99,20 @@ def tile_causalwaveletfieldattentionbyte_pa_kernel(tc, x, k_w, k_b, v_w, v_b, sc
             for j in range(2, NS - 1):
                 kk = 3 * 2 ** (j - 2)
                 nc.vector.tensor_copy(out=rows[:, :, kk:kk + 1], in_=thr2[:, j, :].unsqueeze(2))
+            nc.vector.tensor_copy(out=kvb_v[:, :, 0, :], in_=kbias[:].rearrange("p (r c) -> p r c", c=P))
+            nc.vector.tensor_copy(out=kvb_v[:, :, 1, :], in_=vbias[:].rearrange("p (r c) -> p r c", c=P))
 
-        def toeplitz_out():
-            nc.sync.dma_start(out=flat[0:P * period].rearrange("(a w) -> a w", w=period), in_=toep[:])
-
-        def toeplitz_back():
+        def toeplitz_out(g0, g1):
             nc.sync.dma_start(
-                out=toep[:, 0:used],
-                in_=flat[0:P * (period - 1)].rearrange("(a w) -> a w", w=period - 1)[:, 0:used],
+                out=flat[g0 * P * GROUP:g1 * P * GROUP].rearrange("(g a w) -> a g w", a=P, w=GROUP),
+                in_=toep[:, g0 * GROUP:g1 * GROUP].rearrange("p (g w) -> p g w", w=GROUP),
+            )
+
+        def toeplitz_back(gi):
+            used = 3 * ROW + 2 * P
+            nc.sync.dma_start(
+                out=toep[:, gi * GROUP:gi * GROUP + used],
+                in_=flat[gi * P * GROUP:gi * P * GROUP + P * (GROUP - 1)].rearrange("(a w) -> a w", w=GROUP - 1)[:, 0:used],
             )
 
         xq = const.tile([P, 2 * B * N], U32, align_bytes=64)
@@ -121,75 +127,81 @@ def tile_causalwaveletfieldattentionbyte_pa_kernel(tc, x, k_w, k_b, v_w, v_b, sc
         field = const.tile([P, 8 * H * 2 * HD], F32)
         field_v = field[:].rearrange("p (q h b c) -> p q h b c", q=8, h=H, b=2)
 
-        def flip_pe(raw):
+        def flip_pe(raw, j, bk):
             raw32 = raw[:].bitcast(F32)
-            pts = []
-            for j in range(4):
-                pt = bank(j)
-                for gu in range(4):
-                    nc.tensor.transpose(pt[:, gu * P:(gu + 1) * P], raw32[:, j * 512 + gu * P:j * 512 + (gu + 1) * P], ident[:])
-                pts.append(pt)
-            return pts
+            pt = bank(bk)
+            for gu in range(4):
+                nc.tensor.transpose(pt[:, gu * P:(gu + 1) * P], raw32[:, j * 512 + gu * P:j * 512 + (gu + 1) * P], ident[:])
+            return pt
 
-        def flip_out(pts, engines):
-            grp = grpp.tile([P, 2 * 2048], BF16, tag="grp", align_bytes=64)
-            grp32 = grp[:].bitcast(F32).rearrange("p (g c u) -> p g c u", g=2, u=2)
-            for j in range(4):
-                src = pts[j][:].rearrange("p (g u c) -> p g c u", g=2, u=2)
-                dst = grp32[:, :, j * P:(j + 1) * P, :]
-                if engines[j] == "s":
-                    nc.scalar.copy(out=dst, in_=src)
-                else:
-                    nc.vector.tensor_copy(out=dst, in_=src)
-            return grp
+        def flip_out(pt, grp, width, slot, engine):
+            grp32 = grp[:, 0:8 * width].bitcast(F32).rearrange("p (g c u) -> p g c u", g=2, u=2)
+            src = pt[:].rearrange("p (g u c) -> p g c u", g=2, u=2)
+            dst = grp32[:, :, slot * P:(slot + 1) * P, :]
+            if engine == "s":
+                nc.scalar.copy(out=dst, in_=src)
+            else:
+                nc.vector.tensor_copy(out=dst, in_=src)
 
-        def quantise(grp, codes, scales, c0):
+        def quantise(grp, width, codes, scales, c0):
             for gg in range(2):
                 nc.vector.quantize_mx(
-                    out=codes[:, gg, c0:c0 + 512].bitcast(FP8X4),
-                    scales=scales[:, gg, c0:c0 + 512],
-                    in_=grp[:, gg * 2048:(gg + 1) * 2048],
+                    out=codes[:, gg, c0:c0 + width].bitcast(FP8X4),
+                    scales=scales[:, gg, c0:c0 + width],
+                    in_=grp[:, gg * 4 * width:(gg + 1) * 4 * width],
                 )
 
-        def proj_pe(t, hh, b0):
-            pair = (bank(b0), bank(b0 + 1))
-            for ps, base in zip(pair, (0, C)):
-                w0 = base + hh * 512
+        def proj_pe(pr, ub, bk):
+            ps = bank(bk)
+            for ti in range(2):
+                t = 2 * ub + ti
                 for gg in range(2):
                     nc.tensor.matmul_mx(
-                        out=ps[:],
+                        out=ps[:, ti * 256:(ti + 1) * 256],
                         lhsT=xq_v[:, gg, t * P:(t + 1) * P].bitcast(FP8X4),
                         lhsT_scale=xs_v[:, gg, t * P:(t + 1) * P],
-                        rhs=wq_v[:, gg, w0:w0 + 512].bitcast(FP8X4),
-                        rhs_scale=ws_v[:, gg, w0:w0 + 512],
+                        rhs=wq_v[:, gg, pr * 256:(pr + 1) * 256].bitcast(FP8X4),
+                        rhs_scale=ws_v[:, gg, pr * 256:(pr + 1) * 256],
                         start=(gg == 0),
                         stop=(gg == 1),
                     )
-            return pair
+            return ps
 
-        def proj_v(pair, hh):
-            kb = work.tile([P, 512], F32, tag="kb")
-            nc.vector.tensor_tensor(out=kb[:], in0=pair[0][:], in1=kbias[:, hh * 512:(hh + 1) * 512], op=ALU.add)
-            vb = work.tile([P, 512], F32, tag="vb")
-            nc.vector.tensor_tensor(out=vb[:], in0=pair[1][:], in1=vbias[:, hh * 512:(hh + 1) * 512], op=ALU.add)
-            return kb, vb
+        def proj_v(ps, pr):
+            kv = work.tile([P, 512], F32, tag="kv")
+            nc.vector.tensor_tensor(
+                out=kv[:].rearrange("p (t c) -> p t c", t=2),
+                in0=ps[:].rearrange("p (t c) -> p t c", t=2),
+                in1=kvb[:, pr * 256:(pr + 1) * 256].unsqueeze(1).to_broadcast([P, 2, 256]),
+                op=ALU.add,
+            )
+            return kv
 
-        def proj_s(kb):
-            msq = small.tile([P, 8], F32, tag="msq")
-            for i in range(8):
-                nc.scalar.activation(
-                    out=kb[:, i * HD:(i + 1) * HD], in_=kb[:, i * HD:(i + 1) * HD], func=ACT.Square,
-                    accum_out=msq[:, i:i + 1],
-                )
-            mag = small.tile([P, 8], F32, tag="mag")
+        def proj_sq(kv):
+            msq = small.tile([P, 4], F32, tag="msq")
+            for ti in range(2):
+                for hl in range(2):
+                    lo = ti * 256 + hl * HD
+                    nc.scalar.activation(
+                        out=kv[:, lo:lo + HD], in_=kv[:, lo:lo + HD], func=ACT.Square,
+                        accum_out=msq[:, 2 * ti + hl:2 * ti + hl + 1],
+                    )
+            return msq
+
+        def proj_sqrt(msq):
+            mag = small.tile([P, 4], F32, tag="mag")
             nc.scalar.activation(out=mag[:], in_=msq[:], func=ACT.Sqrt)
             return mag
 
-        def proj_g(t, hh, vb, mag):
+        def proj_s(kv):
+            return proj_sqrt(proj_sq(kv))
+
+        def proj_g(pr, ub, kv, mag):
+            t = 2 * ub
             nc.gpsimd.tensor_tensor(
-                out=field_v[:, t % 8, hh * 8:(hh + 1) * 8, t // 8, :],
-                in0=vb[:].rearrange("p (h c) -> p h c", c=HD),
-                in1=mag[:].unsqueeze(2).to_broadcast([P, 8, HD]),
+                out=field_v[:, t % 8:t % 8 + 2, 2 * pr:2 * pr + 2, t // 8, :],
+                in0=kv[:].rearrange("p (t m h c) -> p t m h c", t=2, m=2, h=2)[:, :, 1, :, :],
+                in1=mag[:].rearrange("p (t h) -> p t h", t=2).unsqueeze(3).to_broadcast([P, 2, 2, HD]),
                 op=ALU.mult,
             )
 
@@ -210,135 +222,273 @@ def tile_causalwaveletfieldattentionbyte_pa_kernel(tc, x, k_w, k_b, v_w, v_b, sc
                 nc.tensor.transpose(f1[:, r * P:(r + 1) * P], stat(h, 4 + r), ident[:])
             return f0, f1
 
-        def filt_m0(h, b0):
-            o0 = bank(b0)
-            for r in range(4):
-                nc.tensor.matmul(o0[:, r * P:(r + 1) * P], lhsT=stat(h, r), rhs=toep[:, h * ROW:h * ROW + P], start=True, stop=True)
-            return o0
+        def filt_m(h, o0, o1, i):
+            near = toep[:, h * ROW:h * ROW + P]
+            far = toep[:, h * ROW + P:h * ROW + 2 * P]
+            if i < 4:
+                nc.tensor.matmul(o0[:, i * P:(i + 1) * P], lhsT=stat(h, i), rhs=near, start=True, stop=True)
+            else:
+                r = (i - 4) // 2
+                if i % 2 == 0:
+                    nc.tensor.matmul(o1[:, r * P:(r + 1) * P], lhsT=stat(h, r), rhs=far, start=True, stop=False)
+                else:
+                    nc.tensor.matmul(o1[:, r * P:(r + 1) * P], lhsT=stat(h, 4 + r), rhs=near, start=False, stop=True)
 
-        def filt_m1(h, o1, rs):
-            for r in rs:
-                nc.tensor.matmul(o1[:, r * P:(r + 1) * P], lhsT=stat(h, r), rhs=toep[:, h * ROW + P:h * ROW + 2 * P], start=True, stop=False)
-                nc.tensor.matmul(o1[:, r * P:(r + 1) * P], lhsT=stat(h, 4 + r), rhs=toep[:, h * ROW:h * ROW + P], start=False, stop=True)
+        TAPS = ((2, pow2, 1), (3, thr2, 0), (6, thr2, 1), (1, pow2, 0))
 
-        def filt_one(h, f0, f1):
-            one = accp.tile([P, N + 8], F32, tag="one")
-            nc.scalar.activation(out=tok(one[:, 1:513]), in_=planes(f0[:]), func=ACT.Copy, scale=pow2[:, 0, h:h + 1])
-            nc.scalar.activation(out=tok(one[:, 513:N + 1]), in_=planes(f1[:]), func=ACT.Copy, scale=pow2[:, 0, h:h + 1])
-            return one
-
-        def filt_acc():
-            acc = accp.tile([P, N + 8], F32, tag="acc")
-            nc.gpsimd.memset(acc[:, N:N + 8], 0.0)
-            return acc
-
-        def tap(h, acc, f, half, which):
-            o, coef = ((2, pow2[:, 1, h:h + 1]), (3, thr2[:, 0, h:h + 1]), (6, thr2[:, 1, h:h + 1]))[which]
-            lo = half * 512 + o
+        def tap(h, acc, f, which):
+            o, table, j = TAPS[which]
             nc.vector.scalar_tensor_tensor(
-                out=tok(acc[:, lo:lo + 512]), in0=planes(f[:]), scalar=coef, in1=tok(acc[:, lo:lo + 512]),
+                out=tok(acc[:, o:o + HALF]), in0=planes(f[:]), scalar=table[:, j, h:h + 1], in1=tok(acc[:, o:o + HALF]),
                 op0=ALU.mult, op1=ALU.add,
             )
 
-        def filt_end(h, acc, one):
-            nc.gpsimd.tensor_tensor(out=acc[:, 1:N], in0=acc[:, 1:N], in1=one[:, 1:N], op=ALU.add)
-            nc.sync.dma_start(out=out[0, h * HD:(h + 1) * HD, :], in_=acc[0:HD, 0:N])
-            nc.sync.dma_start(out=out[1, h * HD:(h + 1) * HD, :], in_=acc[HD:P, 0:N])
+        def store(h, acc, half):
+            for b in range(2):
+                nc.sync.dma_start(
+                    out=out[b, h * HD:(h + 1) * HD, half * HALF:(half + 1) * HALF], in_=acc[b * HD:(b + 1) * HD, 0:HALF]
+                )
 
-        raws = [load_x(0, 0), load_w(k_w, 0), load_w(v_w, 0), load_x(0, 1)]
+        raws = {}
+        raws["x0"] = load_x(0)
+        raws["w0"] = load_w(0)
+        raws["x1"] = load_x(1)
+        raws["x2"] = load_x(2)
         gains()
-        spots = ((xq_v, xs_v, 0), (wq_v, ws_v, 0), (wq_v, ws_v, C), (xq_v, xs_v, 512), (xq_v, xs_v, 1024),
-                 (xq_v, xs_v, 1536), (wq_v, ws_v, 512), (wq_v, ws_v, C + 512))
-        later = (lambda: load_x(1, 0), lambda: load_x(1, 1), lambda: load_w(k_w, 1), lambda: load_w(v_w, 1))
-        grps = []
 
-        def chunk(c, engines):
-            pts = flip_pe(raws[c])
-            if c < 4:
-                raws.append(later[c]())
-            if c == 3:
-                toeplitz_out()
-                toeplitz_back()
-            grps.append(flip_out(pts, engines))
+        def x_chunk_pe(ch):
+            return [flip_pe(raws["x%d" % ch], j, j) for j in range(4)]
 
-        def quant(c):
-            quantise(grps[c], spots[c][0], spots[c][1], spots[c][2])
+        def x_chunk_out(pts, engines):
+            grp = grpp.tile([P, 4096], BF16, tag="grp", align_bytes=64)
+            for j in range(4):
+                flip_out(pts[j], grp, 512, j, engines[j])
+            return grp
 
-        def unit_tail(t, hh, pair):
-            kb, vb = proj_v(pair, hh)
-            mag = proj_s(kb)
-            proj_g(t, hh, vb, mag)
+        wgrp = {}
 
-        chunk(0, "svsv")
-        chunk(1, "svsv")
-        quant(0)
-        chunk(2, "svsv")
-        quant(1)
-        chunk(3, "svsv")
-        quant(2)
-        for c in range(4):
-            pend = []
-            for t in range(4 * c, 4 * c + 4):
-                pend.append((t, proj_pe(t, 0, 4 + 2 * (t % 2))))
-                if len(pend) == 2:
-                    unit_tail(pend[0][0], 0, pend[0][1])
-                    pend = pend[1:]
-                if t == 4 * c + 1:
-                    quant(c + 3)
-            chunk(c + 4, "svsv")
-            unit_tail(pend[0][0], 0, pend[0][1])
-        quant(7)
+        def w_tile_pe(pr, m, bk):
+            return flip_pe(raws["w%d" % (pr // 2)], 2 * m + pr % 2, bk)
 
-        state = {}
+        def w_tile_out(pr, m, pt, engine):
+            if m == 0:
+                wgrp[pr] = grpp.tile([P, 2048], BF16, tag="wgrp", align_bytes=64, name="wgrp")
+            flip_out(pt, wgrp[pr], 256, m, engine)
 
-        def head_front(h, fb, ob):
-            f0, f1 = filt_t(h, fb)
-            o0 = filt_m0(h, ob)
-            o1 = bank(ob + 1)
-            state[h] = [f0, f1, o0, o1, None, None]
+        def w_quant(pr):
+            quantise(wgrp[pr], 256, wq_v, ws_v, pr * 256)
 
-        def head_scalar0(h):
-            f0, f1, o0, o1 = state[h][0:4]
-            acc = filt_acc()
-            state[h][4] = acc
-            state[h][5] = filt_one(h, f0, f1)
-            nc.scalar.copy(out=tok(acc[:, 0:512]), in_=planes(o0[:]))
+        pend_v, pend_s, pend_g = [], [], []
 
-        def head_scalar1(h):
-            nc.scalar.copy(out=tok(state[h][4][:, 512:N]), in_=planes(state[h][3][:]))
+        def take(queue):
+            first = queue[0]
+            queue[:] = queue[1:]
+            return first
 
-        def head_taps(h, part):
-            f0, f1, o0, o1, acc, one = state[h]
-            for which, half in (((0, 0), (0, 1), (1, 0)), ((1, 1), (2, 0), (2, 1)))[part]:
-                tap(h, acc, (f0, f1)[half], half, which)
+        def ensure_free(bk):
+            while any(e[3] == bk for e in pend_v):
+                pr, ub, ps, used_bank = take(pend_v)
+                pend_s.append((pr, ub, proj_v(ps, pr)))
 
-        for i in range(8):
-            head_front(i, 2 * (i % 2), 4)
-            pa = proj_pe(2 * i, 1, 6)
-            if i > 0:
-                head_taps(i - 1, 0)
-            kb, vb = proj_v(pa, 1)
-            head_scalar0(i)
-            mag = proj_s(kb)
-            proj_g(2 * i, 1, vb, mag)
-            filt_m1(i, state[i][3], (0, 1))
-            pb = proj_pe(2 * i + 1, 1, 6)
-            if i > 0:
-                head_taps(i - 1, 1)
-                filt_end(i - 1, state[i - 1][4], state[i - 1][5])
-            kb, vb = proj_v(pb, 1)
-            filt_m1(i, state[i][3], (2, 3))
-            head_scalar1(i)
-            mag = proj_s(kb)
-            proj_g(2 * i + 1, 1, vb, mag)
-        for h in range(8, H):
-            head_front(h, 2 * (h % 2), 4 + 2 * (h % 2))
-            head_taps(h - 1, 0)
-            head_scalar0(h)
-            filt_m1(h, state[h][3], (0, 1, 2, 3))
-            head_taps(h - 1, 1)
-            filt_end(h - 1, state[h - 1][4], state[h - 1][5])
-            head_scalar1(h)
-        head_taps(H - 1, 0)
-        head_taps(H - 1, 1)
-        filt_end(H - 1, state[H - 1][4], state[H - 1][5])
+        def unit(pr, ub, bk):
+            ensure_free(bk)
+            pend_v.append((pr, ub, proj_pe(pr, ub, bk), bk))
+
+        def drain(limit_v, limit_s, limit_g):
+            while len(pend_v) > limit_v:
+                pr, ub, ps, used_bank = take(pend_v)
+                pend_s.append((pr, ub, proj_v(ps, pr)))
+            while len(pend_s) > limit_s:
+                pr, ub, kv = take(pend_s)
+                pend_g.append((pr, ub, kv, proj_s(kv)))
+            while len(pend_g) > limit_g:
+                pr, ub, kv, mag = take(pend_g)
+                proj_g(pr, ub, kv, mag)
+
+        LEAD = 4
+        units = [(pr, ub) for pr in range(8) for ub in range(8)]
+        wtiles = [(pr, m) for pr in range(3, 8) for m in range(2)]
+        nb = [6, 7, 4, 5]
+        cnt = [0]
+
+        def pro_unit():
+            pr, ub = take(units)
+            unit(pr, ub, nb[cnt[0] % 4])
+            cnt[0] += 1
+            drain(1, 1, 1)
+
+        p0 = x_chunk_pe(0)
+        raws["x3"] = load_x(3)
+        toeplitz_out(0, 1)
+        wk = w_tile_pe(0, 0, 4)
+        wv = w_tile_pe(0, 1, 5)
+        g0 = x_chunk_out(p0, "svsv")
+        w_tile_out(0, 0, wk, "s")
+        w_tile_out(0, 1, wv, "v")
+        p1 = x_chunk_pe(1)
+        raws["w1"] = load_w(1)
+        toeplitz_back(0)
+        toeplitz_out(1, 4)
+        quantise(g0, 512, xq_v, xs_v, 0)
+        w_quant(0)
+        g1 = x_chunk_out(p1, "svsv")
+        pro_unit()
+        quantise(g1, 512, xq_v, xs_v, 512)
+        pro_unit()
+        p2 = x_chunk_pe(2)
+        g2 = x_chunk_out(p2, "svsv")
+        pro_unit()
+        quantise(g2, 512, xq_v, xs_v, 1024)
+        pro_unit()
+        p3 = x_chunk_pe(3)
+        g3 = x_chunk_out(p3, "svsv")
+        pro_unit()
+        quantise(g3, 512, xq_v, xs_v, 1536)
+        pro_unit()
+        wk = w_tile_pe(1, 0, 0)
+        wv = w_tile_pe(1, 1, 1)
+        raws["w2"] = load_w(2)
+        w_tile_out(1, 0, wk, "s")
+        w_tile_out(1, 1, wv, "v")
+        wk = w_tile_pe(2, 0, 2)
+        wv = w_tile_pe(2, 1, 3)
+        pro_unit()
+        w_quant(1)
+        w_tile_out(2, 0, wk, "s")
+        w_tile_out(2, 1, wv, "v")
+        pro_unit()
+        w_quant(2)
+        for i in range(LEAD):
+            pro_unit()
+        for gi in range(1, 4):
+            toeplitz_back(gi)
+
+        st = {}
+        ring = [6, 7]
+        rc = [0]
+
+        def next_bank():
+            rc[0] += 1
+            return ring[rc[0] % 2]
+
+        MSPLIT = ((0, 2), (2, 5), (5, 8), (8, 11), (11, 12))
+        ON_VECTOR = (H - 1,)
+
+        def ok(h):
+            return 0 <= h < H
+
+        def v_tap(h, half, which):
+            if ok(h):
+                tap(h, st[h]["acc"][half], st[h]["f"][half], which)
+
+        def s_evac(h, half):
+            if ok(h):
+                nc.scalar.copy(out=tok(st[h]["acc"][half][:, 0:HALF]), in_=planes(st[h]["o"][half][:]))
+
+        def s_one(h, half):
+            if ok(h) and h not in ON_VECTOR:
+                if half == 0:
+                    st[h]["one"] = accp.tile([P, N + PAD], F32, tag="one", bufs=2, name="one")
+                lo = half * HALF + 1
+                nc.scalar.activation(
+                    out=tok(st[h]["one"][:, lo:lo + HALF]), in_=planes(st[h]["f"][half][:]), func=ACT.Copy,
+                    scale=pow2[:, 0, h:h + 1],
+                )
+
+        def finish(h, half):
+            if not ok(h):
+                return
+            acc, one = st[h]["acc"], st[h]["one"]
+            eng = nc.vector if h in ON_VECTOR else nc.gpsimd
+            if half == 1:
+                eng.tensor_tensor(out=acc[1][:, 0:PAD], in0=acc[1][:, 0:PAD], in1=acc[0][:, HALF:HALF + PAD], op=ALU.add)
+            if h not in ON_VECTOR:
+                if half == 0:
+                    eng.tensor_tensor(out=acc[0][:, 1:HALF], in0=acc[0][:, 1:HALF], in1=one[:, 1:HALF], op=ALU.add)
+                else:
+                    eng.tensor_tensor(out=acc[1][:, 0:HALF], in0=acc[1][:, 0:HALF], in1=one[:, HALF:N], op=ALU.add)
+            store(h, acc[half], half)
+
+        def v_add():
+            if pend_v:
+                pr, ub, ps, used_bank = take(pend_v)
+                pend_s.append((pr, ub, proj_v(ps, pr)))
+
+        def s_unit(other):
+            if pend_s:
+                pr, ub, kv = take(pend_s)
+                msq = proj_sq(kv)
+                other()
+                pend_g.append((pr, ub, kv, proj_sqrt(msq)))
+            else:
+                other()
+
+        def g_unit():
+            if pend_g:
+                pr, ub, kv, mag = take(pend_g)
+                proj_g(pr, ub, kv, mag)
+
+        for h in range(H + 2):
+            live = h < H
+            has_w = live and len(wtiles) > 0
+            wpt = None
+            wpr, wm = take(wtiles) if has_w else (0, 0)
+            if live:
+                f0, f1 = filt_t(h, 2 * (h % 2))
+                acc_a = accp.tile([P, HALF + PAD], F32, tag="acca")
+                acc_b = accp.tile([P, HALF + PAD], F32, tag="accb")
+                nc.gpsimd.memset(acc_a[:, HALF:HALF + PAD], 0.0)
+                nc.gpsimd.memset(acc_b[:, HALF:HALF + PAD], 0.0)
+                ensure_free(4)
+                st[h] = {"f": (f0, f1), "o": [bank(4), None], "acc": (acc_a, acc_b), "one": None}
+                if has_w:
+                    wb = next_bank()
+                    ensure_free(wb)
+                    wpt = w_tile_pe(wpr, wm, wb)
+                    if (wpr, wm) == (3, 1):
+                        raws["w3"] = load_w(3)
+            for p in range(5):
+                g_unit()
+                if p == 0:
+                    s_evac(h - 1, 1)
+                    if h - 2 not in ON_VECTOR:
+                        finish(h - 2, 1)
+                if live:
+                    if p == 1:
+                        ensure_free(5)
+                        st[h]["o"][1] = bank(5)
+                    for i in range(MSPLIT[p][0], MSPLIT[p][1]):
+                        filt_m(h, st[h]["o"][0], st[h]["o"][1], i)
+                    if units and p < 4:
+                        upr, uub = take(units)
+                        unit(upr, uub, next_bank())
+                if len(pend_v) > 1 or not units:
+                    v_add()
+                last = h - 1 in ON_VECTOR
+                if p == 0:
+                    v_tap(h - 1, 0, 1)
+                    v_tap(h - 1, 1, 0)
+                    s_unit(lambda: w_tile_out(wpr, wm, wpt, "s") if has_w else None)
+                elif p == 1:
+                    v_tap(h - 1, 0, 2)
+                    if last:
+                        v_tap(h - 1, 1, 1)
+                        v_tap(h - 1, 0, 3)
+                    s_unit(lambda: s_one(h, 0))
+                elif p == 2:
+                    finish(h - 1, 0)
+                    if last:
+                        v_tap(h - 1, 1, 2)
+                    else:
+                        v_tap(h - 1, 1, 1)
+                    s_unit(lambda: s_evac(h, 0))
+                elif p == 3:
+                    if last:
+                        v_tap(h - 1, 1, 3)
+                        finish(h - 1, 1)
+                    else:
+                        v_tap(h - 1, 1, 2)
+                    v_tap(h, 0, 0)
+                    if has_w and wm == 1:
+                        w_quant(wpr)
+                    s_unit(lambda: s_one(h, 1))

@@ -28,10 +28,10 @@ def tile_causalwaveletfieldattentionbyte_pa_kernel(tc, x, k_w, k_b, v_w, v_b, sc
     with ExitStack() as ctx:
         const = ctx.enter_context(tc.tile_pool(name="const", bufs=1))
         rawp = ctx.enter_context(tc.tile_pool(name="rawp", bufs=4))
-        grpp = ctx.enter_context(tc.tile_pool(name="grpp", bufs=2))
+        grpp = ctx.enter_context(tc.tile_pool(name="grpp", bufs=4))
         work = ctx.enter_context(tc.tile_pool(name="work", bufs=4))
         small = ctx.enter_context(tc.tile_pool(name="small", bufs=6))
-        accp = ctx.enter_context(tc.tile_pool(name="accp", bufs=3))
+        accp = ctx.enter_context(tc.tile_pool(name="accp", bufs=4))
         psum = ctx.enter_context(tc.psum_pool(name="psum", bufs=1))
         ctx.enter_context(tc.manual_schedule())
 
@@ -43,19 +43,15 @@ def tile_causalwaveletfieldattentionbyte_pa_kernel(tc, x, k_w, k_b, v_w, v_b, sc
 
         sg_bf = const.tile([P, NS * H], BF16)
         nc.scalar.dma_start(out=sg_bf[:], in_=scale_gain.rearrange("j h -> (j h)").partition_broadcast(P))
-        kbias = const.tile([P, C], BF16)
-        nc.scalar.dma_start(out=kbias[:], in_=k_b.partition_broadcast(P))
-        vbias = const.tile([P, C], BF16)
-        nc.scalar.dma_start(out=vbias[:], in_=v_b.partition_broadcast(P))
+        biases = grpp.tile([P, 2 * C], BF16, tag="wgrp", align_bytes=64)
+        nc.scalar.dma_start(out=biases[:, 0:C], in_=k_b.partition_broadcast(P))
+        nc.scalar.dma_start(out=biases[:, C:2 * C], in_=v_b.partition_broadcast(P))
         kvb = const.tile([P, 2 * C], BF16)
-        kvb_v = kvb[:].rearrange("p (r m c) -> p r m c", m=2, c=P)
 
-        def load_x(ch):
-            raw = rawp.tile([P, 4 * D], BF16, tag="rawx", bufs=3)
-            nc.sync.dma_start(
-                out=raw[:].rearrange("p (r d) -> p r d", r=4),
-                in_=x[ch // 2, (ch % 2) * HALF:(ch % 2 + 1) * HALF, :].rearrange("(a r) d -> a r d", r=4),
-            )
+        def load_x(ub):
+            raw = rawp.tile([P, 2 * D], BF16, tag="rawx", bufs=6)
+            half = x[ub // 4, ((ub // 2) % 2) * HALF:((ub // 2) % 2 + 1) * HALF, :].rearrange("(a r) d -> a r d", r=4)
+            nc.sync.dma_start(out=raw[:].rearrange("p (r d) -> p r d", r=2), in_=half[:, 2 * (ub % 2):2 * (ub % 2) + 2, :])
             return raw
 
         def load_w(ch):
@@ -64,6 +60,11 @@ def tile_causalwaveletfieldattentionbyte_pa_kernel(tc, x, k_w, k_b, v_w, v_b, sc
             nc.sync.dma_start(out=view[:, 0:2, :], in_=k_w[ch * 256:(ch + 1) * 256, :].rearrange("(i p) d -> p i d", p=P))
             nc.sync.dma_start(out=view[:, 2:4, :], in_=v_w[ch * 256:(ch + 1) * 256, :].rearrange("(i p) d -> p i d", p=P))
             return raw
+
+        def load_w_pair(raw, pr):
+            for m, w in enumerate((k_w, v_w)):
+                j = 2 * m + pr % 2
+                nc.sync.dma_start(out=raw[:, j * D:(j + 1) * D], in_=w[pr * P:(pr + 1) * P, :])
 
         g = const.tile([P, NS, H], F32)
         gmax = const.tile([P, H], F32)
@@ -99,8 +100,12 @@ def tile_causalwaveletfieldattentionbyte_pa_kernel(tc, x, k_w, k_b, v_w, v_b, sc
             for j in range(2, NS - 1):
                 kk = 3 * 2 ** (j - 2)
                 nc.vector.tensor_copy(out=rows[:, :, kk:kk + 1], in_=thr2[:, j, :].unsqueeze(2))
-            nc.vector.tensor_copy(out=kvb_v[:, :, 0, :], in_=kbias[:].rearrange("p (r c) -> p r c", c=P))
-            nc.vector.tensor_copy(out=kvb_v[:, :, 1, :], in_=vbias[:].rearrange("p (r c) -> p r c", c=P))
+
+        def pair_biases():
+            nc.vector.tensor_copy(
+                out=kvb[:].rearrange("p (r m c) -> p m r c", m=2, c=P),
+                in_=biases[:].rearrange("p (m r c) -> p m r c", m=2, c=P),
+            )
 
         def toeplitz_out(g0, g1):
             nc.sync.dma_start(
@@ -243,27 +248,59 @@ def tile_causalwaveletfieldattentionbyte_pa_kernel(tc, x, k_w, k_b, v_w, v_b, sc
                 op0=ALU.mult, op1=ALU.add,
             )
 
+        def tap_part(h, acc, f, which, part):
+            o, table, j = TAPS[which]
+            lo = o + part * 256
+            nc.vector.scalar_tensor_tensor(
+                out=tok(acc[:, lo:lo + 256]), in0=planes(f[:])[:, part * 64:(part + 1) * 64, :], scalar=table[:, j, h:h + 1],
+                in1=tok(acc[:, lo:lo + 256]), op0=ALU.mult, op1=ALU.add,
+            )
+
         def store(h, acc, half):
             for b in range(2):
                 nc.sync.dma_start(
                     out=out[b, h * HD:(h + 1) * HD, half * HALF:(half + 1) * HALF], in_=acc[b * HD:(b + 1) * HD, 0:HALF]
                 )
 
-        raws = {}
-        raws["x0"] = load_x(0)
-        raws["w0"] = load_w(0)
-        raws["x1"] = load_x(1)
-        raws["x2"] = load_x(2)
-        gains()
+        pend_v, pend_s, pend_g = [], [], []
 
-        def x_chunk_pe(ch):
-            return [flip_pe(raws["x%d" % ch], j, j) for j in range(4)]
+        def take(queue):
+            first = queue[0]
+            queue[:] = queue[1:]
+            return first
 
-        def x_chunk_out(pts, engines):
-            grp = grpp.tile([P, 4096], BF16, tag="grp", align_bytes=64)
-            for j in range(4):
-                flip_out(pts[j], grp, 512, j, engines[j])
-            return grp
+        def v_add():
+            pr, ub, ps, used_bank = take(pend_v)
+            pend_s.append((pr, ub, proj_v(ps, pr)))
+
+        def ensure_free(bk):
+            while any(e[3] == bk for e in pend_v):
+                v_add()
+
+        def unit(pr, ub, bk):
+            ensure_free(bk)
+            pend_v.append((pr, ub, proj_pe(pr, ub, bk), bk))
+
+        def s_unit(other):
+            pr, ub, kv = take(pend_s)
+            msq = proj_sq(kv)
+            other()
+            pend_g.append((pr, ub, kv, proj_sqrt(msq)))
+
+        def g_unit():
+            pr, ub, kv, mag = take(pend_g)
+            proj_g(pr, ub, kv, mag)
+
+        def nothing():
+            return None
+
+        ringp = [0]
+
+        def pbank():
+            bk = ringp[0] % 8
+            ringp[0] += 1
+            ensure_free(bk)
+            return bk
 
         wgrp = {}
 
@@ -278,101 +315,93 @@ def tile_causalwaveletfieldattentionbyte_pa_kernel(tc, x, k_w, k_b, v_w, v_b, sc
         def w_quant(pr):
             quantise(wgrp[pr], 256, wq_v, ws_v, pr * 256)
 
-        pend_v, pend_s, pend_g = [], [], []
+        def x_tiles_pe(ch):
+            return [flip_pe(raws["x%d" % ch], j, pbank()) for j in range(4)]
 
-        def take(queue):
-            first = queue[0]
-            queue[:] = queue[1:]
-            return first
+        def x_tiles_out(pts, engines):
+            grp = grpp.tile([P, 4096], BF16, tag="grp", align_bytes=64)
+            for j in range(4):
+                flip_out(pts[j], grp, 512, j, engines[j])
+            return grp
 
-        def ensure_free(bk):
-            while any(e[3] == bk for e in pend_v):
-                pr, ub, ps, used_bank = take(pend_v)
-                pend_s.append((pr, ub, proj_v(ps, pr)))
+        raws = {}
+        raws["w0"] = rawp.tile([P, 4 * D], BF16, tag="raww", bufs=2, name="raww")
+        load_w_pair(raws["w0"], 0)
+        xraw = [load_x(ub) for ub in range(6)]
+        gains()
+        xgrp = {}
+        xpt = {}
 
-        def unit(pr, ub, bk):
-            ensure_free(bk)
-            pend_v.append((pr, ub, proj_pe(pr, ub, bk), bk))
+        def x_pe(ub):
+            xpt[ub] = [flip_pe(xraw[ub], j, pbank()) for j in range(2)]
 
-        def drain(limit_v, limit_s, limit_g):
-            while len(pend_v) > limit_v:
-                pr, ub, ps, used_bank = take(pend_v)
-                pend_s.append((pr, ub, proj_v(ps, pr)))
-            while len(pend_s) > limit_s:
+        def x_out(ub, engines):
+            xgrp[ub] = grpp.tile([P, 2048], BF16, tag="wgrp", align_bytes=64, name="xgrp")
+            for j in range(2):
+                flip_out(xpt[ub][j], xgrp[ub], 256, j, engines[j])
+
+        def x_quant(ub):
+            quantise(xgrp[ub], 256, xq_v, xs_v, ub * 256)
+
+        wt = [w_tile_pe(0, m, pbank()) for m in range(2)]
+        w_tile_out(0, 0, wt[0], "s")
+        w_tile_out(0, 1, wt[1], "s")
+        lagged = []
+        for k in range(8 + 7):
+            if k < 8:
+                x_pe(k)
+                if k < 2:
+                    xraw.append(load_x(6 + k))
+                if k == 1:
+                    load_w_pair(raws["w0"], 1)
+                    toeplitz_out(0, 1)
+                    raws["w1"] = load_w(1)
+            if k == 8:
+                wt = [w_tile_pe(1, m, pbank()) for m in range(2)]
+            if k == 9:
+                wt = wt + [w_tile_pe(2, m, pbank()) for m in range(2)]
+                raws["w2"] = load_w(2)
+            if k == 4:
+                toeplitz_back(0)
+                toeplitz_out(1, 4)
+            if 0 <= k - 3 < 8:
+                unit(0, k - 3, pbank())
+            if 0 <= k - 1 < 8:
+                x_out(k - 1, ["ss","ss","ss","ss","ss","ss","sv","sv"][k - 1])
+            if k == 0:
+                w_quant(0)
+                pair_biases()
+            if len(pend_v) > 1 or (k - 3 >= 7 and pend_v):
+                v_add()
+            if 0 <= k - 1 < 8:
+                x_quant(k - 1)
+            if lagged:
+                pr, ub, kv, msq = take(lagged)
+                pend_g.append((pr, ub, kv, proj_sqrt(msq)))
+            if len(pend_s) > 1 or (k - 3 >= 8 and pend_s):
                 pr, ub, kv = take(pend_s)
-                pend_g.append((pr, ub, kv, proj_s(kv)))
-            while len(pend_g) > limit_g:
-                pr, ub, kv, mag = take(pend_g)
-                proj_g(pr, ub, kv, mag)
-
-        LEAD = 4
-        units = [(pr, ub) for pr in range(8) for ub in range(8)]
-        wtiles = [(pr, m) for pr in range(3, 8) for m in range(2)]
-        nb = [6, 7, 4, 5]
-        cnt = [0]
-
-        def pro_unit():
-            pr, ub = take(units)
-            unit(pr, ub, nb[cnt[0] % 4])
-            cnt[0] += 1
-            drain(1, 1, 1)
-
-        p0 = x_chunk_pe(0)
-        raws["x3"] = load_x(3)
-        toeplitz_out(0, 1)
-        wk = w_tile_pe(0, 0, 4)
-        wv = w_tile_pe(0, 1, 5)
-        g0 = x_chunk_out(p0, "svsv")
-        w_tile_out(0, 0, wk, "s")
-        w_tile_out(0, 1, wv, "v")
-        p1 = x_chunk_pe(1)
-        raws["w1"] = load_w(1)
-        toeplitz_back(0)
-        toeplitz_out(1, 4)
-        quantise(g0, 512, xq_v, xs_v, 0)
-        w_quant(0)
-        g1 = x_chunk_out(p1, "svsv")
-        pro_unit()
-        quantise(g1, 512, xq_v, xs_v, 512)
-        pro_unit()
-        p2 = x_chunk_pe(2)
-        g2 = x_chunk_out(p2, "svsv")
-        pro_unit()
-        quantise(g2, 512, xq_v, xs_v, 1024)
-        pro_unit()
-        p3 = x_chunk_pe(3)
-        g3 = x_chunk_out(p3, "svsv")
-        pro_unit()
-        quantise(g3, 512, xq_v, xs_v, 1536)
-        pro_unit()
-        wk = w_tile_pe(1, 0, 0)
-        wv = w_tile_pe(1, 1, 1)
-        raws["w2"] = load_w(2)
-        w_tile_out(1, 0, wk, "s")
-        w_tile_out(1, 1, wv, "v")
-        wk = w_tile_pe(2, 0, 2)
-        wv = w_tile_pe(2, 1, 3)
-        pro_unit()
+                msq = proj_sq(kv)
+                if k - 3 >= 8:
+                    pend_g.append((pr, ub, kv, proj_sqrt(msq)))
+                else:
+                    lagged.append((pr, ub, kv, msq))
+            while pend_g:
+                g_unit()
+        w_tile_out(1, 0, wt[0], "v")
+        w_tile_out(1, 1, wt[1], "s")
         w_quant(1)
-        w_tile_out(2, 0, wk, "s")
-        w_tile_out(2, 1, wv, "v")
-        pro_unit()
+        w_tile_out(2, 0, wt[2], "v")
+        w_tile_out(2, 1, wt[3], "s")
         w_quant(2)
-        for i in range(LEAD):
-            pro_unit()
         for gi in range(1, 4):
             toeplitz_back(gi)
 
+        units = [(pr, ub) for pr in range(1, 8) for ub in range(8)]
+        wtiles = [(pr, m) for pr in range(3, 8) for m in range(2)]
         st = {}
-        ring = [6, 7]
         rc = [0]
-
-        def next_bank():
-            rc[0] += 1
-            return ring[rc[0] % 2]
-
         MSPLIT = ((0, 2), (2, 5), (5, 8), (8, 11), (11, 12))
-        ON_VECTOR = (H - 1,)
+        LAST = H - 1
 
         def ok(h):
             return 0 <= h < H
@@ -386,9 +415,9 @@ def tile_causalwaveletfieldattentionbyte_pa_kernel(tc, x, k_w, k_b, v_w, v_b, sc
                 nc.scalar.copy(out=tok(st[h]["acc"][half][:, 0:HALF]), in_=planes(st[h]["o"][half][:]))
 
         def s_one(h, half):
-            if ok(h) and h not in ON_VECTOR:
+            if ok(h):
                 if half == 0:
-                    st[h]["one"] = accp.tile([P, N + PAD], F32, tag="one", bufs=2, name="one")
+                    st[h]["one"] = accp.tile([P, N + PAD], F32, tag="one", bufs=3, name="one")
                 lo = half * HALF + 1
                 nc.scalar.activation(
                     out=tok(st[h]["one"][:, lo:lo + HALF]), in_=planes(st[h]["f"][half][:]), func=ACT.Copy,
@@ -399,96 +428,125 @@ def tile_causalwaveletfieldattentionbyte_pa_kernel(tc, x, k_w, k_b, v_w, v_b, sc
             if not ok(h):
                 return
             acc, one = st[h]["acc"], st[h]["one"]
-            eng = nc.vector if h in ON_VECTOR else nc.gpsimd
-            if half == 1:
-                eng.tensor_tensor(out=acc[1][:, 0:PAD], in0=acc[1][:, 0:PAD], in1=acc[0][:, HALF:HALF + PAD], op=ALU.add)
-            if h not in ON_VECTOR:
-                if half == 0:
-                    eng.tensor_tensor(out=acc[0][:, 1:HALF], in0=acc[0][:, 1:HALF], in1=one[:, 1:HALF], op=ALU.add)
-                else:
-                    eng.tensor_tensor(out=acc[1][:, 0:HALF], in0=acc[1][:, 0:HALF], in1=one[:, HALF:N], op=ALU.add)
+            if half == 0:
+                nc.gpsimd.tensor_tensor(out=acc[0][:, 1:HALF], in0=acc[0][:, 1:HALF], in1=one[:, 1:HALF], op=ALU.add)
+            else:
+                nc.gpsimd.tensor_tensor(out=acc[1][:, 0:PAD], in0=acc[1][:, 0:PAD], in1=acc[0][:, HALF:HALF + PAD], op=ALU.add)
+                nc.gpsimd.tensor_tensor(out=acc[1][:, 0:HALF], in0=acc[1][:, 0:HALF], in1=one[:, HALF:N], op=ALU.add)
             store(h, acc[half], half)
 
-        def v_add():
-            if pend_v:
-                pr, ub, ps, used_bank = take(pend_v)
-                pend_s.append((pr, ub, proj_v(ps, pr)))
+        def open_head(h, fb):
+            ensure_free(fb)
+            ensure_free(fb + 1)
+            f0, f1 = filt_t(h, fb)
+            acc_a = accp.tile([P, HALF + PAD], F32, tag="acca")
+            acc_b = accp.tile([P, HALF + PAD], F32, tag="accb")
+            nc.gpsimd.memset(acc_a[:, HALF:HALF + PAD], 0.0)
+            nc.gpsimd.memset(acc_b[:, HALF:HALF + PAD], 0.0)
+            ensure_free(4)
+            st[h] = {"f": (f0, f1), "o": [bank(4), None], "acc": (acc_a, acc_b), "one": None}
 
-        def s_unit(other):
-            if pend_s:
-                pr, ub, kv = take(pend_s)
-                msq = proj_sq(kv)
-                other()
-                pend_g.append((pr, ub, kv, proj_sqrt(msq)))
-            else:
-                other()
+        def matmuls(h, lo, hi):
+            for i in range(lo, hi):
+                if i == 4:
+                    ensure_free(5)
+                    st[h]["o"][1] = bank(5)
+                filt_m(h, st[h]["o"][0], st[h]["o"][1], i)
 
-        def g_unit():
-            if pend_g:
-                pr, ub, kv, mag = take(pend_g)
-                proj_g(pr, ub, kv, mag)
+        def last_start():
+            acc_b, f1 = st[LAST]["acc"][1], st[LAST]["f"][1]
+            nc.scalar.activation(
+                out=acc_b[:, 0:1], in_=st[LAST]["f"][0][:, HALF - 1:HALF], func=ACT.Copy, scale=pow2[:, 0, LAST:LAST + 1]
+            )
+            nc.scalar.activation(
+                out=tok(acc_b[:, 1:HALF + 1]), in_=planes(f1[:]), func=ACT.Copy, scale=pow2[:, 0, LAST:LAST + 1]
+            )
 
-        for h in range(H + 2):
+        def last_end():
+            acc_a, acc_b = st[LAST]["acc"]
+            one = st[LAST]["one"]
+            v_tap(LAST, 0, 2)
+            nc.gpsimd.tensor_tensor(out=acc_a[:, 1:HALF], in0=acc_a[:, 1:HALF], in1=one[:, 1:HALF], op=ALU.add)
+            store(LAST, acc_a, 0)
+            nc.vector.tensor_tensor(
+                out=tok(acc_b[:, 0:HALF]), in0=planes(st[LAST]["o"][1][:]), in1=tok(acc_b[:, 0:HALF]), op=ALU.add
+            )
+            nc.vector.tensor_tensor(out=acc_b[:, 0:PAD], in0=acc_b[:, 0:PAD], in1=acc_a[:, HALF:HALF + PAD], op=ALU.add)
+            store(LAST, acc_b, 1)
+
+        for h in range(H + 1):
             live = h < H
+            ring = (6, 7, 2, 3) if h == 0 else (6, 7)
+            quota = 2 if h == 0 else 1
             has_w = live and len(wtiles) > 0
             wpt = None
             wpr, wm = take(wtiles) if has_w else (0, 0)
             if live:
-                f0, f1 = filt_t(h, 2 * (h % 2))
-                acc_a = accp.tile([P, HALF + PAD], F32, tag="acca")
-                acc_b = accp.tile([P, HALF + PAD], F32, tag="accb")
-                nc.gpsimd.memset(acc_a[:, HALF:HALF + PAD], 0.0)
-                nc.gpsimd.memset(acc_b[:, HALF:HALF + PAD], 0.0)
-                ensure_free(4)
-                st[h] = {"f": (f0, f1), "o": [bank(4), None], "acc": (acc_a, acc_b), "one": None}
-                if has_w:
-                    wb = next_bank()
-                    ensure_free(wb)
-                    wpt = w_tile_pe(wpr, wm, wb)
-                    if (wpr, wm) == (3, 1):
-                        raws["w3"] = load_w(3)
+                open_head(h, 2 * (h % 2) if h < 14 else (6, 0)[h - 14])
+            if has_w:
+                rc[0] += 1
+                wb = ring[rc[0] % len(ring)]
+                ensure_free(wb)
+                wpt = w_tile_pe(wpr, wm, wb)
+                if (wpr, wm) == (3, 1):
+                    raws["w3"] = load_w(3)
             for p in range(5):
-                g_unit()
+                n_s = len(pend_s)
+                for i in range(len(pend_g)):
+                    g_unit()
                 if p == 0:
-                    s_evac(h - 1, 1)
-                    if h - 2 not in ON_VECTOR:
-                        finish(h - 2, 1)
+                    if h - 1 != LAST:
+                        s_evac(h - 1, 1)
+                    finish(h - 2, 1)
+                fresh = 0
                 if live:
-                    if p == 1:
-                        ensure_free(5)
-                        st[h]["o"][1] = bank(5)
-                    for i in range(MSPLIT[p][0], MSPLIT[p][1]):
-                        filt_m(h, st[h]["o"][0], st[h]["o"][1], i)
-                    if units and p < 4:
-                        upr, uub = take(units)
-                        unit(upr, uub, next_bank())
-                if len(pend_v) > 1 or not units:
+                    matmuls(h, MSPLIT[p][0], MSPLIT[p][1])
+                    if p < 4:
+                        for i in range(quota):
+                            if units:
+                                upr, uub = take(units)
+                                rc[0] += 1
+                                unit(upr, uub, ring[rc[0] % len(ring)])
+                                fresh += 1
+                while len(pend_v) > fresh:
                     v_add()
-                last = h - 1 in ON_VECTOR
-                if p == 0:
+                other = nothing
+                if h == H:
+                    if p == 0:
+                        last_end()
+                elif p == 0:
+                    if has_w:
+                        other = lambda: w_tile_out(wpr, wm, wpt, "s")
+                    if h == LAST:
+                        other = last_start
                     v_tap(h - 1, 0, 1)
                     v_tap(h - 1, 1, 0)
-                    s_unit(lambda: w_tile_out(wpr, wm, wpt, "s") if has_w else None)
                 elif p == 1:
+                    other = lambda: s_one(h, 0)
                     v_tap(h - 1, 0, 2)
-                    if last:
-                        v_tap(h - 1, 1, 1)
-                        v_tap(h - 1, 0, 3)
-                    s_unit(lambda: s_one(h, 0))
+                    if h == LAST:
+                        v_tap(h, 1, 0)
                 elif p == 2:
+                    other = lambda: s_evac(h, 0)
                     finish(h - 1, 0)
-                    if last:
-                        v_tap(h - 1, 1, 2)
-                    else:
-                        v_tap(h - 1, 1, 1)
-                    s_unit(lambda: s_evac(h, 0))
+                    v_tap(h - 1, 1, 1)
+                    if h == LAST:
+                        v_tap(h, 1, 1)
                 elif p == 3:
-                    if last:
-                        v_tap(h - 1, 1, 3)
-                        finish(h - 1, 1)
-                    else:
+                    if h != LAST:
+                        other = lambda: s_one(h, 1)
+                    if units or pend_v:
                         v_tap(h - 1, 1, 2)
-                    v_tap(h, 0, 0)
+                        v_tap(h, 0, 0)
+                    else:
+                        v_tap(h, 0, 0)
+                        v_tap(h - 1, 1, 2)
+                    if h == LAST:
+                        v_tap(h, 0, 1)
+                        v_tap(h, 1, 2)
                     if has_w and wm == 1:
                         w_quant(wpr)
-                    s_unit(lambda: s_one(h, 1))
+                if n_s == 0:
+                    other()
+                for i in range(n_s):
+                    s_unit(other if i == 0 else nothing)

@@ -15,11 +15,18 @@ AX = mybir.AxisListType
 P = 128
 B, N, D, C, H, NS = 2, 1024, 1024, 1024, 16, 10
 HD = C // H
+HALF = N // 2
 T0, T1, T2, T3 = (0.4829629131445341, 0.8365163037378079, 0.2241438680420134, -0.1294095225512604)
+
+PAIRS = H // 2
+UNITS = 8 * PAIRS
+AHEAD = 12
+EARLY_PAIRS = 3
 ROW = 320
 GROUP = 4 * ROW
-HALF = N // 2
 PAD = 8
+SHIFTS = ((2, 0, 1), (3, 1, 0), (6, 1, 1))
+
 FLOPS = 2 * (B * N) * D * (2 * C)
 
 
@@ -27,7 +34,7 @@ def tile_causalwaveletfieldattentionbyte_pa_kernel(tc, x, k_w, k_b, v_w, v_b, sc
     nc = tc.nc
     with ExitStack() as ctx:
         const = ctx.enter_context(tc.tile_pool(name="const", bufs=1))
-        rawp = ctx.enter_context(tc.tile_pool(name="rawp", bufs=4))
+        rawp = ctx.enter_context(tc.tile_pool(name="rawp", bufs=6))
         grpp = ctx.enter_context(tc.tile_pool(name="grpp", bufs=4))
         work = ctx.enter_context(tc.tile_pool(name="work", bufs=4))
         small = ctx.enter_context(tc.tile_pool(name="small", bufs=6))
@@ -43,28 +50,10 @@ def tile_causalwaveletfieldattentionbyte_pa_kernel(tc, x, k_w, k_b, v_w, v_b, sc
 
         sg_bf = const.tile([P, NS * H], BF16)
         nc.scalar.dma_start(out=sg_bf[:], in_=scale_gain.rearrange("j h -> (j h)").partition_broadcast(P))
-        biases = grpp.tile([P, 2 * C], BF16, tag="wgrp", align_bytes=64)
+        biases = grpp.tile([P, 2 * C], BF16, tag="grp", align_bytes=64)
         nc.scalar.dma_start(out=biases[:, 0:C], in_=k_b.partition_broadcast(P))
         nc.scalar.dma_start(out=biases[:, C:2 * C], in_=v_b.partition_broadcast(P))
-        kvb = const.tile([P, 2 * C], BF16)
-
-        def load_x(ub):
-            raw = rawp.tile([P, 2 * D], BF16, tag="rawx", bufs=6)
-            half = x[ub // 4, ((ub // 2) % 2) * HALF:((ub // 2) % 2 + 1) * HALF, :].rearrange("(a r) d -> a r d", r=4)
-            nc.sync.dma_start(out=raw[:].rearrange("p (r d) -> p r d", r=2), in_=half[:, 2 * (ub % 2):2 * (ub % 2) + 2, :])
-            return raw
-
-        def load_w(ch):
-            raw = rawp.tile([P, 4 * D], BF16, tag="raww", bufs=2)
-            view = raw[:].rearrange("p (i d) -> p i d", i=4)
-            nc.sync.dma_start(out=view[:, 0:2, :], in_=k_w[ch * 256:(ch + 1) * 256, :].rearrange("(i p) d -> p i d", p=P))
-            nc.sync.dma_start(out=view[:, 2:4, :], in_=v_w[ch * 256:(ch + 1) * 256, :].rearrange("(i p) d -> p i d", p=P))
-            return raw
-
-        def load_w_pair(raw, pr):
-            for m, w in enumerate((k_w, v_w)):
-                j = 2 * m + pr % 2
-                nc.sync.dma_start(out=raw[:, j * D:(j + 1) * D], in_=w[pr * P:(pr + 1) * P, :])
+        pair_bias = const.tile([P, 2 * C], BF16)
 
         g = const.tile([P, NS, H], F32)
         gmax = const.tile([P, H], F32)
@@ -73,12 +62,13 @@ def tile_causalwaveletfieldattentionbyte_pa_kernel(tc, x, k_w, k_b, v_w, v_b, sc
         gone = const.tile([P, H], F32)
         pow2 = const.tile([P, NS, H], F32)
         thr2 = const.tile([P, NS, H], F32)
+        tables = (pow2, thr2)
         toep = const.tile([P, H * ROW], F32)
-        rows = toep[:].rearrange("p (h w) -> p h w", w=ROW)
-        flat = out[1].rearrange("c n -> (c n)")
+        scratch = out[1].rearrange("c n -> (c n)")
 
         def gains():
             by_head = g[:].rearrange("p j h -> p h j")
+            rows = toep[:].rearrange("p (h w) -> p h w", w=ROW)
             nc.vector.memset(toep[:], 0.0)
             nc.vector.tensor_copy(out=g[:], in_=sg_bf[:].rearrange("p (j h) -> p j h", j=NS))
             nc.vector.tensor_reduce(out=gmax[:], in_=by_head, axis=AX.X, op=ALU.max)
@@ -95,30 +85,28 @@ def tile_causalwaveletfieldattentionbyte_pa_kernel(tc, x, k_w, k_b, v_w, v_b, sc
             nc.vector.tensor_reduce(out=gone[:], in_=by_head, axis=AX.X, op=ALU.add)
             nc.vector.tensor_scalar_mul(out=rows[:, :, 0:1], in0=gone[:].unsqueeze(2), scalar1=T3)
             for j in range(2, NS):
-                kk = 2 ** (j - 2)
-                nc.vector.tensor_copy(out=rows[:, :, kk:kk + 1], in_=pow2[:, j, :].unsqueeze(2))
+                col = 2 ** (j - 2)
+                nc.vector.tensor_copy(out=rows[:, :, col:col + 1], in_=pow2[:, j, :].unsqueeze(2))
             for j in range(2, NS - 1):
-                kk = 3 * 2 ** (j - 2)
-                nc.vector.tensor_copy(out=rows[:, :, kk:kk + 1], in_=thr2[:, j, :].unsqueeze(2))
+                col = 3 * 2 ** (j - 2)
+                nc.vector.tensor_copy(out=rows[:, :, col:col + 1], in_=thr2[:, j, :].unsqueeze(2))
 
-        def pair_biases():
+        def sort_biases():
             nc.vector.tensor_copy(
-                out=kvb[:].rearrange("p (r m c) -> p m r c", m=2, c=P),
+                out=pair_bias[:].rearrange("p (r m c) -> p m r c", m=2, c=P),
                 in_=biases[:].rearrange("p (m r c) -> p m r c", m=2, c=P),
             )
 
-        def toeplitz_out(g0, g1):
-            nc.sync.dma_start(
-                out=flat[g0 * P * GROUP:g1 * P * GROUP].rearrange("(g a w) -> a g w", a=P, w=GROUP),
+        def rows_out(queue, g0, g1):
+            queue.dma_start(
+                out=scratch[g0 * P * GROUP:g1 * P * GROUP].rearrange("(g a w) -> a g w", a=P, w=GROUP),
                 in_=toep[:, g0 * GROUP:g1 * GROUP].rearrange("p (g w) -> p g w", w=GROUP),
             )
 
-        def toeplitz_back(gi):
+        def blocks_back(queue, gi):
             used = 3 * ROW + 2 * P
-            nc.sync.dma_start(
-                out=toep[:, gi * GROUP:gi * GROUP + used],
-                in_=flat[gi * P * GROUP:gi * P * GROUP + P * (GROUP - 1)].rearrange("(a w) -> a w", w=GROUP - 1)[:, 0:used],
-            )
+            skewed = scratch[gi * P * GROUP:gi * P * GROUP + P * (GROUP - 1)].rearrange("(a w) -> a w", w=GROUP - 1)
+            queue.dma_start(out=toep[:, gi * GROUP:gi * GROUP + used], in_=skewed[:, 0:used])
 
         xq = const.tile([P, 2 * B * N], U32, align_bytes=64)
         xs = const.tile([P, 2 * B * N], U8, align_bytes=64)
@@ -132,37 +120,59 @@ def tile_causalwaveletfieldattentionbyte_pa_kernel(tc, x, k_w, k_b, v_w, v_b, sc
         field = const.tile([P, 8 * H * 2 * HD], F32)
         field_v = field[:].rearrange("p (q h b c) -> p q h b c", q=8, h=H, b=2)
 
-        def flip_pe(raw, j, bk):
-            raw32 = raw[:].bitcast(F32)
-            pt = bank(bk)
-            for gu in range(4):
-                nc.tensor.transpose(pt[:, gu * P:(gu + 1) * P], raw32[:, j * 512 + gu * P:j * 512 + (gu + 1) * P], ident[:])
-            return pt
+        raw, flipped, grouped = {}, {}, {}
 
-        def flip_out(pt, grp, width, slot, engine):
-            grp32 = grp[:, 0:8 * width].bitcast(F32).rearrange("p (g c u) -> p g c u", g=2, u=2)
-            src = pt[:].rearrange("p (g u c) -> p g c u", g=2, u=2)
-            dst = grp32[:, :, slot * P:(slot + 1) * P, :]
-            if engine == "s":
+        def load_leaf(leaf):
+            kind, i = leaf
+            raw[leaf] = rawp.tile([P, 2 * D], BF16, tag="raw", name="raw")
+            halves = raw[leaf][:].rearrange("p (r d) -> p r d", r=2)
+            if kind == "x":
+                tokens = x[i // 4, ((i // 2) % 2) * HALF:((i // 2) % 2 + 1) * HALF, :].rearrange("(a r) d -> a r d", r=4)
+                nc.sync.dma_start(out=halves, in_=tokens[:, 2 * (i % 2):2 * (i % 2) + 2, :])
+            else:
+                nc.sync.dma_start(out=halves[:, 0, :], in_=k_w[i * P:(i + 1) * P, :])
+                nc.sync.dma_start(out=halves[:, 1, :], in_=v_w[i * P:(i + 1) * P, :])
+
+        def flip(leaf, j, bk):
+            words = raw[leaf][:].bitcast(F32)
+            flipped[leaf, j] = bank(bk)
+            for gu in range(4):
+                nc.tensor.transpose(
+                    flipped[leaf, j][:, gu * P:(gu + 1) * P], words[:, j * 512 + gu * P:j * 512 + (gu + 1) * P], ident[:]
+                )
+
+        def regroup(leaf, j, engine):
+            if j == 0:
+                grouped[leaf] = grpp.tile([P, 2 * C], BF16, tag="grp", align_bytes=64, name="grp")
+            dst = grouped[leaf][:].bitcast(F32).rearrange("p (g c u) -> p g c u", g=2, u=2)[:, :, j * P:(j + 1) * P, :]
+            src = flipped[leaf, j][:].rearrange("p (g u c) -> p g c u", g=2, u=2)
+            if engine == "scalar":
                 nc.scalar.copy(out=dst, in_=src)
             else:
                 nc.vector.tensor_copy(out=dst, in_=src)
 
-        def quantise(grp, width, codes, scales, c0):
+        def quantise(leaf):
+            kind, i = leaf
+            codes, scales = (xq_v, xs_v) if kind == "x" else (wq_v, ws_v)
             for gg in range(2):
                 nc.vector.quantize_mx(
-                    out=codes[:, gg, c0:c0 + width].bitcast(FP8X4),
-                    scales=scales[:, gg, c0:c0 + width],
-                    in_=grp[:, gg * 4 * width:(gg + 1) * 4 * width],
+                    out=codes[:, gg, i * 256:(i + 1) * 256].bitcast(FP8X4),
+                    scales=scales[:, gg, i * 256:(i + 1) * 256],
+                    in_=grouped[leaf][:, gg * C:(gg + 1) * C],
                 )
 
-        def proj_pe(pr, ub, bk):
-            ps = bank(bk)
+        sums, biased, squares, norms = {}, {}, {}, {}
+
+        def project(u, bk):
+            if not 0 <= u < UNITS:
+                return
+            pr = u // 8
+            sums[u] = bank(bk)
             for ti in range(2):
-                t = 2 * ub + ti
+                t = 2 * (u % 8) + ti
                 for gg in range(2):
                     nc.tensor.matmul_mx(
-                        out=ps[:, ti * 256:(ti + 1) * 256],
+                        out=sums[u][:, ti * 256:(ti + 1) * 256],
                         lhsT=xq_v[:, gg, t * P:(t + 1) * P].bitcast(FP8X4),
                         lhsT_scale=xs_v[:, gg, t * P:(t + 1) * P],
                         rhs=wq_v[:, gg, pr * 256:(pr + 1) * 256].bitcast(FP8X4),
@@ -170,383 +180,208 @@ def tile_causalwaveletfieldattentionbyte_pa_kernel(tc, x, k_w, k_b, v_w, v_b, sc
                         start=(gg == 0),
                         stop=(gg == 1),
                     )
-            return ps
 
-        def proj_v(ps, pr):
-            kv = work.tile([P, 512], F32, tag="kv")
+        def add_bias(u):
+            if not 0 <= u < UNITS:
+                return
+            pr = u // 8
+            biased[u] = work.tile([P, 512], F32, tag="kv", name="kv")
             nc.vector.tensor_tensor(
-                out=kv[:].rearrange("p (t c) -> p t c", t=2),
-                in0=ps[:].rearrange("p (t c) -> p t c", t=2),
-                in1=kvb[:, pr * 256:(pr + 1) * 256].unsqueeze(1).to_broadcast([P, 2, 256]),
+                out=biased[u][:].rearrange("p (t c) -> p t c", t=2),
+                in0=sums[u][:].rearrange("p (t c) -> p t c", t=2),
+                in1=pair_bias[:, pr * 256:(pr + 1) * 256].unsqueeze(1).to_broadcast([P, 2, 256]),
                 op=ALU.add,
             )
-            return kv
 
-        def proj_sq(kv):
-            msq = small.tile([P, 4], F32, tag="msq")
-            for ti in range(2):
-                for hl in range(2):
-                    lo = ti * 256 + hl * HD
-                    nc.scalar.activation(
-                        out=kv[:, lo:lo + HD], in_=kv[:, lo:lo + HD], func=ACT.Square,
-                        accum_out=msq[:, 2 * ti + hl:2 * ti + hl + 1],
-                    )
-            return msq
+        def square(u):
+            if not 0 <= u < UNITS:
+                return
+            squares[u] = small.tile([P, 4], F32, tag="msq", name="msq")
+            for th in range(4):
+                lo = (th // 2) * 256 + (th % 2) * HD
+                nc.scalar.activation(
+                    out=biased[u][:, lo:lo + HD], in_=biased[u][:, lo:lo + HD], func=ACT.Square,
+                    accum_out=squares[u][:, th:th + 1],
+                )
 
-        def proj_sqrt(msq):
-            mag = small.tile([P, 4], F32, tag="mag")
-            nc.scalar.activation(out=mag[:], in_=msq[:], func=ACT.Sqrt)
-            return mag
+        def root(u):
+            if not 0 <= u < UNITS:
+                return
+            norms[u] = small.tile([P, 4], F32, tag="mag", name="mag")
+            nc.scalar.activation(out=norms[u][:], in_=squares[u][:], func=ACT.Sqrt)
 
-        def proj_s(kv):
-            return proj_sqrt(proj_sq(kv))
-
-        def proj_g(pr, ub, kv, mag):
-            t = 2 * ub
+        def make_field(u):
+            if not 0 <= u < UNITS:
+                return
+            pr, t = u // 8, 2 * (u % 8)
             nc.gpsimd.tensor_tensor(
                 out=field_v[:, t % 8:t % 8 + 2, 2 * pr:2 * pr + 2, t // 8, :],
-                in0=kv[:].rearrange("p (t m h c) -> p t m h c", t=2, m=2, h=2)[:, :, 1, :, :],
-                in1=mag[:].rearrange("p (t h) -> p t h", t=2).unsqueeze(3).to_broadcast([P, 2, 2, HD]),
+                in0=biased[u][:].rearrange("p (t m h c) -> p t m h c", t=2, m=2, h=2)[:, :, 1, :, :],
+                in1=norms[u][:].rearrange("p (t h) -> p t h", t=2).unsqueeze(3).to_broadcast([P, 2, 2, HD]),
                 op=ALU.mult,
             )
 
-        def tok(ap):
+        def in_order(ap):
             return ap.rearrange("p (a r) -> p a r", r=4)
 
         def planes(ap):
             return ap.rearrange("p (r a) -> p a r", r=4)
 
-        def stat(h, q):
+        def stationary(h, q):
             return field_v[:, q, h, :, :].rearrange("p b c -> p (b c)")
 
-        def filt_t(h, b0):
-            f0, f1 = bank(b0), bank(b0 + 1)
-            for r in range(4):
-                nc.tensor.transpose(f0[:, r * P:(r + 1) * P], stat(h, r), ident[:])
-            for r in range(4):
-                nc.tensor.transpose(f1[:, r * P:(r + 1) * P], stat(h, 4 + r), ident[:])
-            return f0, f1
+        copy_f, toeplitz, acc, first_tap = {}, {}, {}, {}
 
-        def filt_m(h, o0, o1, i):
+        def open_head(h):
+            for half in range(2):
+                copy_f[h, half] = bank(2 * (h % 2) + half)
+                for r in range(4):
+                    nc.tensor.transpose(copy_f[h, half][:, r * P:(r + 1) * P], stationary(h, 4 * half + r), ident[:])
+            for half in range(2):
+                acc[h, half] = accp.tile([P, HALF + PAD], F32, tag="acc%d" % half, name="acc")
+                nc.gpsimd.memset(acc[h, half][:, HALF:HALF + PAD], 0.0)
+
+        def filter_matmul(h, i):
             near = toep[:, h * ROW:h * ROW + P]
             far = toep[:, h * ROW + P:h * ROW + 2 * P]
+            if i == 0 or i == 4:
+                toeplitz[h, i // 4] = bank(4 + i // 4)
             if i < 4:
-                nc.tensor.matmul(o0[:, i * P:(i + 1) * P], lhsT=stat(h, i), rhs=near, start=True, stop=True)
+                nc.tensor.matmul(toeplitz[h, 0][:, i * P:(i + 1) * P], lhsT=stationary(h, i), rhs=near, start=True, stop=True)
             else:
                 r = (i - 4) // 2
+                dst = toeplitz[h, 1][:, r * P:(r + 1) * P]
                 if i % 2 == 0:
-                    nc.tensor.matmul(o1[:, r * P:(r + 1) * P], lhsT=stat(h, r), rhs=far, start=True, stop=False)
+                    nc.tensor.matmul(dst, lhsT=stationary(h, r), rhs=far, start=True, stop=False)
                 else:
-                    nc.tensor.matmul(o1[:, r * P:(r + 1) * P], lhsT=stat(h, 4 + r), rhs=near, start=False, stop=True)
+                    nc.tensor.matmul(dst, lhsT=stationary(h, 4 + r), rhs=near, start=False, stop=True)
 
-        TAPS = ((2, pow2, 1), (3, thr2, 0), (6, thr2, 1), (1, pow2, 0))
+        def empty_toeplitz(h, half):
+            if 0 <= h < H:
+                nc.scalar.copy(out=in_order(acc[h, half][:, 0:HALF]), in_=planes(toeplitz[h, half][:]))
 
-        def tap(h, acc, f, which):
-            o, table, j = TAPS[which]
+        def shift_one(h, half):
+            if not 0 <= h < H:
+                return
+            if half == 0:
+                first_tap[h] = accp.tile([P, N + PAD], F32, tag="one", bufs=3, name="one")
+            lo = half * HALF + 1
+            nc.scalar.activation(
+                out=in_order(first_tap[h][:, lo:lo + HALF]), in_=planes(copy_f[h, half][:]), func=ACT.Copy,
+                scale=pow2[:, 0, h:h + 1],
+            )
+
+        def tap(h, half, which):
+            if not 0 <= h < H:
+                return
+            shift, table, j = SHIFTS[which]
+            window = in_order(acc[h, half][:, shift:shift + HALF])
             nc.vector.scalar_tensor_tensor(
-                out=tok(acc[:, o:o + HALF]), in0=planes(f[:]), scalar=table[:, j, h:h + 1], in1=tok(acc[:, o:o + HALF]),
+                out=window, in0=planes(copy_f[h, half][:]), scalar=tables[table][:, j, h:h + 1], in1=window,
                 op0=ALU.mult, op1=ALU.add,
             )
 
-        def tap_part(h, acc, f, which, part):
-            o, table, j = TAPS[which]
-            lo = o + part * 256
-            nc.vector.scalar_tensor_tensor(
-                out=tok(acc[:, lo:lo + 256]), in0=planes(f[:])[:, part * 64:(part + 1) * 64, :], scalar=table[:, j, h:h + 1],
-                in1=tok(acc[:, lo:lo + 256]), op0=ALU.mult, op1=ALU.add,
-            )
-
-        def store(h, acc, half):
+        def finish(h, half):
+            if not 0 <= h < H:
+                return
+            a0, a1, one = acc[h, 0], acc[h, 1], first_tap[h]
+            if half == 0:
+                nc.gpsimd.tensor_tensor(out=a0[:, 1:HALF], in0=a0[:, 1:HALF], in1=one[:, 1:HALF], op=ALU.add)
+            else:
+                nc.gpsimd.tensor_tensor(out=a1[:, 0:PAD], in0=a1[:, 0:PAD], in1=a0[:, HALF:HALF + PAD], op=ALU.add)
+                nc.gpsimd.tensor_tensor(out=a1[:, 0:HALF], in0=a1[:, 0:HALF], in1=one[:, HALF:N], op=ALU.add)
             for b in range(2):
                 nc.sync.dma_start(
-                    out=out[b, h * HD:(h + 1) * HD, half * HALF:(half + 1) * HALF], in_=acc[b * HD:(b + 1) * HD, 0:HALF]
+                    out=out[b, h * HD:(h + 1) * HD, half * HALF:(half + 1) * HALF],
+                    in_=acc[h, half][b * HD:(b + 1) * HD, 0:HALF],
                 )
 
-        pend_v, pend_s, pend_g = [], [], []
-
-        def take(queue):
-            first = queue[0]
-            queue[:] = queue[1:]
-            return first
-
-        def v_add():
-            pr, ub, ps, used_bank = take(pend_v)
-            pend_s.append((pr, ub, proj_v(ps, pr)))
-
-        def ensure_free(bk):
-            while any(e[3] == bk for e in pend_v):
-                v_add()
-
-        def unit(pr, ub, bk):
-            ensure_free(bk)
-            pend_v.append((pr, ub, proj_pe(pr, ub, bk), bk))
-
-        def s_unit(other):
-            pr, ub, kv = take(pend_s)
-            msq = proj_sq(kv)
-            other()
-            pend_g.append((pr, ub, kv, proj_sqrt(msq)))
-
-        def g_unit():
-            pr, ub, kv, mag = take(pend_g)
-            proj_g(pr, ub, kv, mag)
-
-        def nothing():
-            return None
-
-        ringp = [0]
-
-        def pbank():
-            bk = ringp[0] % 8
-            ringp[0] += 1
-            ensure_free(bk)
-            return bk
-
-        wgrp = {}
-
-        def w_tile_pe(pr, m, bk):
-            return flip_pe(raws["w%d" % (pr // 2)], 2 * m + pr % 2, bk)
-
-        def w_tile_out(pr, m, pt, engine):
-            if m == 0:
-                wgrp[pr] = grpp.tile([P, 2048], BF16, tag="wgrp", align_bytes=64, name="wgrp")
-            flip_out(pt, wgrp[pr], 256, m, engine)
-
-        def w_quant(pr):
-            quantise(wgrp[pr], 256, wq_v, ws_v, pr * 256)
-
-        def x_tiles_pe(ch):
-            return [flip_pe(raws["x%d" % ch], j, pbank()) for j in range(4)]
-
-        def x_tiles_out(pts, engines):
-            grp = grpp.tile([P, 4096], BF16, tag="grp", align_bytes=64)
-            for j in range(4):
-                flip_out(pts[j], grp, 512, j, engines[j])
-            return grp
-
-        raws = {}
-        raws["w0"] = rawp.tile([P, 4 * D], BF16, tag="raww", bufs=2, name="raww")
-        load_w_pair(raws["w0"], 0)
-        xraw = [load_x(ub) for ub in range(6)]
+        leaves = [("w", 0)] + [("x", i) for i in range(8)] + [("w", pr) for pr in range(1, PAIRS)]
+        early = 8 + EARLY_PAIRS
+        for leaf in leaves[0:6]:
+            load_leaf(leaf)
         gains()
-        xgrp = {}
-        xpt = {}
-
-        def x_pe(ub):
-            xpt[ub] = [flip_pe(xraw[ub], j, pbank()) for j in range(2)]
-
-        def x_out(ub, engines):
-            xgrp[ub] = grpp.tile([P, 2048], BF16, tag="wgrp", align_bytes=64, name="xgrp")
-            for j in range(2):
-                flip_out(xpt[ub][j], xgrp[ub], 256, j, engines[j])
-
-        def x_quant(ub):
-            quantise(xgrp[ub], 256, xq_v, xs_v, ub * 256)
-
-        wt = [w_tile_pe(0, m, pbank()) for m in range(2)]
-        w_tile_out(0, 0, wt[0], "s")
-        w_tile_out(0, 1, wt[1], "s")
-        lagged = []
-        for k in range(8 + 7):
-            if k < 8:
-                x_pe(k)
-                if k < 2:
-                    xraw.append(load_x(6 + k))
-                if k == 1:
-                    load_w_pair(raws["w0"], 1)
-                    toeplitz_out(0, 1)
-                    raws["w1"] = load_w(1)
-            if k == 8:
-                wt = [w_tile_pe(1, m, pbank()) for m in range(2)]
-            if k == 9:
-                wt = wt + [w_tile_pe(2, m, pbank()) for m in range(2)]
-                raws["w2"] = load_w(2)
-            if k == 4:
-                toeplitz_back(0)
-                toeplitz_out(1, 4)
-            if 0 <= k - 3 < 8:
-                unit(0, k - 3, pbank())
-            if 0 <= k - 1 < 8:
-                x_out(k - 1, ["ss","ss","ss","ss","ss","ss","sv","sv"][k - 1])
-            if k == 0:
-                w_quant(0)
-                pair_biases()
-            if len(pend_v) > 1 or (k - 3 >= 7 and pend_v):
-                v_add()
-            if 0 <= k - 1 < 8:
-                x_quant(k - 1)
-            if lagged:
-                pr, ub, kv, msq = take(lagged)
-                pend_g.append((pr, ub, kv, proj_sqrt(msq)))
-            if len(pend_s) > 1 or (k - 3 >= 8 and pend_s):
-                pr, ub, kv = take(pend_s)
-                msq = proj_sq(kv)
-                if k - 3 >= 8:
-                    pend_g.append((pr, ub, kv, proj_sqrt(msq)))
-                else:
-                    lagged.append((pr, ub, kv, msq))
-            while pend_g:
-                g_unit()
-        w_tile_out(1, 0, wt[0], "v")
-        w_tile_out(1, 1, wt[1], "s")
-        w_quant(1)
-        w_tile_out(2, 0, wt[2], "v")
-        w_tile_out(2, 1, wt[3], "s")
-        w_quant(2)
+        rows_out(nc.gpsimd, 0, 1)
+        blocks_back(nc.gpsimd, 0)
+        turn = 0
+        for s in range(AHEAD + 4):
+            if s < early:
+                flip(leaves[s], 0, turn % 8)
+                flip(leaves[s], 1, (turn + 1) % 8)
+                turn += 2
+                if s + 6 < len(leaves):
+                    load_leaf(leaves[s + 6])
+            if s >= 4:
+                project(s - 4, turn % 8)
+                turn += 1
+            square(s - 6)
+            root(s - 7)
+            make_field(s - 7)
+            if 1 <= s <= early:
+                regroup(leaves[s - 1], 0, "scalar")
+                regroup(leaves[s - 1], 1, "scalar" if s % 2 == 1 else "vector")
+            add_bias(s - 5)
+            if 1 <= s <= early:
+                quantise(leaves[s - 1])
+            if s == 1:
+                sort_biases()
+        add_bias(AHEAD - 1)
+        rows_out(nc.sync, 1, 4)
         for gi in range(1, 4):
-            toeplitz_back(gi)
+            blocks_back(nc.sync, gi)
 
-        units = [(pr, ub) for pr in range(1, 8) for ub in range(8)]
-        wtiles = [(pr, m) for pr in range(3, 8) for m in range(2)]
-        st = {}
-        rc = [0]
-        MSPLIT = ((0, 2), (2, 5), (5, 8), (8, 11), (11, 12))
-        LAST = H - 1
-
-        def ok(h):
-            return 0 <= h < H
-
-        def v_tap(h, half, which):
-            if ok(h):
-                tap(h, st[h]["acc"][half], st[h]["f"][half], which)
-
-        def s_evac(h, half):
-            if ok(h):
-                nc.scalar.copy(out=tok(st[h]["acc"][half][:, 0:HALF]), in_=planes(st[h]["o"][half][:]))
-
-        def s_one(h, half):
-            if ok(h):
-                if half == 0:
-                    st[h]["one"] = accp.tile([P, N + PAD], F32, tag="one", bufs=3, name="one")
-                lo = half * HALF + 1
-                nc.scalar.activation(
-                    out=tok(st[h]["one"][:, lo:lo + HALF]), in_=planes(st[h]["f"][half][:]), func=ACT.Copy,
-                    scale=pow2[:, 0, h:h + 1],
-                )
-
-        def finish(h, half):
-            if not ok(h):
-                return
-            acc, one = st[h]["acc"], st[h]["one"]
-            if half == 0:
-                nc.gpsimd.tensor_tensor(out=acc[0][:, 1:HALF], in0=acc[0][:, 1:HALF], in1=one[:, 1:HALF], op=ALU.add)
+        def slot(h, p):
+            u = AHEAD + 4 * h + p
+            if p == 0:
+                empty_toeplitz(h - 1, 1)
+                finish(h - 2, 1)
+            project(u, 6 + u % 2)
+            if u - 1 >= AHEAD:
+                add_bias(u - 1)
+            square(u - 2)
+            root(u - 3)
+            make_field(u - 3)
+            if p == 0:
+                tap(h - 1, 0, 1)
+                tap(h - 1, 1, 0)
+            elif p == 1:
+                shift_one(h, 0)
+                tap(h - 1, 0, 2)
+                late_weights_quantise(h - 1)
+            elif p == 2:
+                empty_toeplitz(h, 0)
+                finish(h - 1, 0)
+                tap(h - 1, 1, 1)
             else:
-                nc.gpsimd.tensor_tensor(out=acc[1][:, 0:PAD], in0=acc[1][:, 0:PAD], in1=acc[0][:, HALF:HALF + PAD], op=ALU.add)
-                nc.gpsimd.tensor_tensor(out=acc[1][:, 0:HALF], in0=acc[1][:, 0:HALF], in1=one[:, HALF:N], op=ALU.add)
-            store(h, acc[half], half)
+                late_weights_out(h)
+                tap(h - 1, 1, 2)
+                tap(h, 0, 0)
+                shift_one(h, 1)
 
-        def open_head(h, fb):
-            ensure_free(fb)
-            ensure_free(fb + 1)
-            f0, f1 = filt_t(h, fb)
-            acc_a = accp.tile([P, HALF + PAD], F32, tag="acca")
-            acc_b = accp.tile([P, HALF + PAD], F32, tag="accb")
-            nc.gpsimd.memset(acc_a[:, HALF:HALF + PAD], 0.0)
-            nc.gpsimd.memset(acc_b[:, HALF:HALF + PAD], 0.0)
-            ensure_free(4)
-            st[h] = {"f": (f0, f1), "o": [bank(4), None], "acc": (acc_a, acc_b), "one": None}
+        def late_leaf(h):
+            return leaves[early + h // 2] if 0 <= h < 2 * (PAIRS - EARLY_PAIRS) else None
 
-        def matmuls(h, lo, hi):
-            for i in range(lo, hi):
-                if i == 4:
-                    ensure_free(5)
-                    st[h]["o"][1] = bank(5)
-                filt_m(h, st[h]["o"][0], st[h]["o"][1], i)
+        def late_weights_in(h):
+            if late_leaf(h) is not None:
+                flip(late_leaf(h), h % 2, 4)
 
-        def last_start():
-            acc_b, f1 = st[LAST]["acc"][1], st[LAST]["f"][1]
-            nc.scalar.activation(
-                out=acc_b[:, 0:1], in_=st[LAST]["f"][0][:, HALF - 1:HALF], func=ACT.Copy, scale=pow2[:, 0, LAST:LAST + 1]
-            )
-            nc.scalar.activation(
-                out=tok(acc_b[:, 1:HALF + 1]), in_=planes(f1[:]), func=ACT.Copy, scale=pow2[:, 0, LAST:LAST + 1]
-            )
+        def late_weights_out(h):
+            if late_leaf(h) is not None:
+                regroup(late_leaf(h), h % 2, "scalar")
 
-        def last_end():
-            acc_a, acc_b = st[LAST]["acc"]
-            one = st[LAST]["one"]
-            v_tap(LAST, 0, 2)
-            nc.gpsimd.tensor_tensor(out=acc_a[:, 1:HALF], in0=acc_a[:, 1:HALF], in1=one[:, 1:HALF], op=ALU.add)
-            store(LAST, acc_a, 0)
-            nc.vector.tensor_tensor(
-                out=tok(acc_b[:, 0:HALF]), in0=planes(st[LAST]["o"][1][:]), in1=tok(acc_b[:, 0:HALF]), op=ALU.add
-            )
-            nc.vector.tensor_tensor(out=acc_b[:, 0:PAD], in0=acc_b[:, 0:PAD], in1=acc_a[:, HALF:HALF + PAD], op=ALU.add)
-            store(LAST, acc_b, 1)
+        def late_weights_quantise(h):
+            if h % 2 == 1 and late_leaf(h) is not None:
+                quantise(late_leaf(h))
 
-        for h in range(H + 1):
-            live = h < H
-            ring = (6, 7, 2, 3) if h == 0 else (6, 7)
-            quota = 2 if h == 0 else 1
-            has_w = live and len(wtiles) > 0
-            wpt = None
-            wpr, wm = take(wtiles) if has_w else (0, 0)
-            if live:
-                open_head(h, 2 * (h % 2) if h < 14 else (6, 0)[h - 14])
-            if has_w:
-                rc[0] += 1
-                wb = ring[rc[0] % len(ring)]
-                ensure_free(wb)
-                wpt = w_tile_pe(wpr, wm, wb)
-                if (wpr, wm) == (3, 1):
-                    raws["w3"] = load_w(3)
-            for p in range(5):
-                n_s = len(pend_s)
-                for i in range(len(pend_g)):
-                    g_unit()
-                if p == 0:
-                    if h - 1 != LAST:
-                        s_evac(h - 1, 1)
-                    finish(h - 2, 1)
-                fresh = 0
-                if live:
-                    matmuls(h, MSPLIT[p][0], MSPLIT[p][1])
-                    if p < 4:
-                        for i in range(quota):
-                            if units:
-                                upr, uub = take(units)
-                                rc[0] += 1
-                                unit(upr, uub, ring[rc[0] % len(ring)])
-                                fresh += 1
-                while len(pend_v) > fresh:
-                    v_add()
-                other = nothing
-                if h == H:
-                    if p == 0:
-                        last_end()
-                elif p == 0:
-                    if has_w:
-                        other = lambda: w_tile_out(wpr, wm, wpt, "s")
-                    if h == LAST:
-                        other = last_start
-                    v_tap(h - 1, 0, 1)
-                    v_tap(h - 1, 1, 0)
-                elif p == 1:
-                    other = lambda: s_one(h, 0)
-                    v_tap(h - 1, 0, 2)
-                    if h == LAST:
-                        v_tap(h, 1, 0)
-                elif p == 2:
-                    other = lambda: s_evac(h, 0)
-                    finish(h - 1, 0)
-                    v_tap(h - 1, 1, 1)
-                    if h == LAST:
-                        v_tap(h, 1, 1)
-                elif p == 3:
-                    if h != LAST:
-                        other = lambda: s_one(h, 1)
-                    if units or pend_v:
-                        v_tap(h - 1, 1, 2)
-                        v_tap(h, 0, 0)
-                    else:
-                        v_tap(h, 0, 0)
-                        v_tap(h - 1, 1, 2)
-                    if h == LAST:
-                        v_tap(h, 0, 1)
-                        v_tap(h, 1, 2)
-                    if has_w and wm == 1:
-                        w_quant(wpr)
-                if n_s == 0:
-                    other()
-                for i in range(n_s):
-                    s_unit(other if i == 0 else nothing)
+        for h in range(H + 2):
+            if h < H:
+                open_head(h)
+                for i in range(12):
+                    filter_matmul(h, i)
+                    if i == 9:
+                        late_weights_in(h)
+                    if i % 3 == 1:
+                        slot(h, i // 3)
+            else:
+                for p in range(4):
+                    slot(h, p)

@@ -22,6 +22,7 @@ PAIRS = H // 2
 UNITS = 8 * PAIRS
 AHEAD = 12
 EARLY_PAIRS = 3
+RAW_BUFS = 6
 ROW = 320
 GROUP = 4 * ROW
 PAD = 8
@@ -34,7 +35,7 @@ def tile_causalwaveletfieldattentionbyte_pa_kernel(tc, x, k_w, k_b, v_w, v_b, sc
     nc = tc.nc
     with ExitStack() as ctx:
         const = ctx.enter_context(tc.tile_pool(name="const", bufs=1))
-        rawp = ctx.enter_context(tc.tile_pool(name="rawp", bufs=6))
+        rawp = ctx.enter_context(tc.tile_pool(name="rawp", bufs=RAW_BUFS))
         grpp = ctx.enter_context(tc.tile_pool(name="grpp", bufs=4))
         work = ctx.enter_context(tc.tile_pool(name="work", bufs=4))
         small = ctx.enter_context(tc.tile_pool(name="small", bufs=6))
@@ -122,10 +123,10 @@ def tile_causalwaveletfieldattentionbyte_pa_kernel(tc, x, k_w, k_b, v_w, v_b, sc
 
         raw, flipped, grouped = {}, {}, {}
 
-        def load_leaf(leaf):
-            kind, i = leaf
-            raw[leaf] = rawp.tile([P, 2 * D], BF16, tag="raw", name="raw")
-            halves = raw[leaf][:].rearrange("p (r d) -> p r d", r=2)
+        def load_slab(slab):
+            kind, i = slab
+            raw[slab] = rawp.tile([P, 2 * D], BF16, tag="raw", name="raw")
+            halves = raw[slab][:].rearrange("p (r d) -> p r d", r=2)
             if kind == "x":
                 tokens = x[i // 4, ((i // 2) % 2) * HALF:((i // 2) % 2 + 1) * HALF, :].rearrange("(a r) d -> a r d", r=4)
                 nc.sync.dma_start(out=halves, in_=tokens[:, 2 * (i % 2):2 * (i % 2) + 2, :])
@@ -133,32 +134,28 @@ def tile_causalwaveletfieldattentionbyte_pa_kernel(tc, x, k_w, k_b, v_w, v_b, sc
                 nc.sync.dma_start(out=halves[:, 0, :], in_=k_w[i * P:(i + 1) * P, :])
                 nc.sync.dma_start(out=halves[:, 1, :], in_=v_w[i * P:(i + 1) * P, :])
 
-        def flip(leaf, j, bk):
-            words = raw[leaf][:].bitcast(F32)
-            flipped[leaf, j] = bank(bk)
+        def flip(slab, j, bk):
+            words = raw[slab][:].bitcast(F32)
+            flipped[slab, j] = bank(bk)
             for gu in range(4):
                 nc.tensor.transpose(
-                    flipped[leaf, j][:, gu * P:(gu + 1) * P], words[:, j * 512 + gu * P:j * 512 + (gu + 1) * P], ident[:]
+                    flipped[slab, j][:, gu * P:(gu + 1) * P], words[:, j * 512 + gu * P:j * 512 + (gu + 1) * P], ident[:]
                 )
 
-        def regroup(leaf, j, engine):
+        def regroup(slab, j):
             if j == 0:
-                grouped[leaf] = grpp.tile([P, 2 * C], BF16, tag="grp", align_bytes=64, name="grp")
-            dst = grouped[leaf][:].bitcast(F32).rearrange("p (g c u) -> p g c u", g=2, u=2)[:, :, j * P:(j + 1) * P, :]
-            src = flipped[leaf, j][:].rearrange("p (g u c) -> p g c u", g=2, u=2)
-            if engine == "scalar":
-                nc.scalar.copy(out=dst, in_=src)
-            else:
-                nc.vector.tensor_copy(out=dst, in_=src)
+                grouped[slab] = grpp.tile([P, 2 * C], BF16, tag="grp", align_bytes=64, name="grp")
+            dst = grouped[slab][:].bitcast(F32).rearrange("p (g c u) -> p g c u", g=2, u=2)[:, :, j * P:(j + 1) * P, :]
+            nc.scalar.copy(out=dst, in_=flipped[slab, j][:].rearrange("p (g u c) -> p g c u", g=2, u=2))
 
-        def quantise(leaf):
-            kind, i = leaf
+        def quantise(slab):
+            kind, i = slab
             codes, scales = (xq_v, xs_v) if kind == "x" else (wq_v, ws_v)
             for gg in range(2):
                 nc.vector.quantize_mx(
                     out=codes[:, gg, i * 256:(i + 1) * 256].bitcast(FP8X4),
                     scales=scales[:, gg, i * 256:(i + 1) * 256],
-                    in_=grouped[leaf][:, gg * C:(gg + 1) * C],
+                    in_=grouped[slab][:, gg * C:(gg + 1) * C],
                 )
 
         sums, biased, squares, norms = {}, {}, {}, {}
@@ -296,39 +293,54 @@ def tile_causalwaveletfieldattentionbyte_pa_kernel(tc, x, k_w, k_b, v_w, v_b, sc
                     in_=acc[h, half][b * HD:(b + 1) * HD, 0:HALF],
                 )
 
-        leaves = [("w", 0)] + [("x", i) for i in range(8)] + [("w", pr) for pr in range(1, PAIRS)]
+        slabs = [("w", 0)] + [("x", i) for i in range(8)] + [("w", pr) for pr in range(1, PAIRS)]
         early = 8 + EARLY_PAIRS
-        for leaf in leaves[0:6]:
-            load_leaf(leaf)
+        for slab in slabs[0:RAW_BUFS]:
+            load_slab(slab)
         gains()
         rows_out(nc.gpsimd, 0, 1)
         blocks_back(nc.gpsimd, 0)
         turn = 0
         for s in range(AHEAD + 4):
             if s < early:
-                flip(leaves[s], 0, turn % 8)
-                flip(leaves[s], 1, (turn + 1) % 8)
+                flip(slabs[s], 0, turn % 8)
+                flip(slabs[s], 1, (turn + 1) % 8)
                 turn += 2
-                if s + 6 < len(leaves):
-                    load_leaf(leaves[s + 6])
+                if s + RAW_BUFS < len(slabs):
+                    load_slab(slabs[s + RAW_BUFS])
             if s >= 4:
                 project(s - 4, turn % 8)
                 turn += 1
+            if 1 <= s <= early:
+                regroup(slabs[s - 1], 0)
+                regroup(slabs[s - 1], 1)
             square(s - 6)
             root(s - 7)
             make_field(s - 7)
-            if 1 <= s <= early:
-                regroup(leaves[s - 1], 0, "scalar")
-                regroup(leaves[s - 1], 1, "scalar" if s % 2 == 1 else "vector")
             add_bias(s - 5)
             if 1 <= s <= early:
-                quantise(leaves[s - 1])
+                quantise(slabs[s - 1])
             if s == 1:
                 sort_biases()
         add_bias(AHEAD - 1)
         rows_out(nc.sync, 1, 4)
         for gi in range(1, 4):
             blocks_back(nc.sync, gi)
+
+        def late_slab(h):
+            return slabs[early + h // 2] if 0 <= h < 2 * (PAIRS - EARLY_PAIRS) else None
+
+        def late_weights_in(h):
+            if late_slab(h) is not None:
+                flip(late_slab(h), h % 2, 4)
+
+        def late_weights_out(h):
+            if late_slab(h) is not None:
+                regroup(late_slab(h), h % 2)
+
+        def late_weights_quantise(h):
+            if h % 2 == 1 and late_slab(h) is not None:
+                quantise(late_slab(h))
 
         def slot(h, p):
             u = AHEAD + 4 * h + p
@@ -357,21 +369,6 @@ def tile_causalwaveletfieldattentionbyte_pa_kernel(tc, x, k_w, k_b, v_w, v_b, sc
                 tap(h - 1, 1, 2)
                 tap(h, 0, 0)
                 shift_one(h, 1)
-
-        def late_leaf(h):
-            return leaves[early + h // 2] if 0 <= h < 2 * (PAIRS - EARLY_PAIRS) else None
-
-        def late_weights_in(h):
-            if late_leaf(h) is not None:
-                flip(late_leaf(h), h % 2, 4)
-
-        def late_weights_out(h):
-            if late_leaf(h) is not None:
-                regroup(late_leaf(h), h % 2, "scalar")
-
-        def late_weights_quantise(h):
-            if h % 2 == 1 and late_leaf(h) is not None:
-                quantise(late_leaf(h))
 
         for h in range(H + 2):
             if h < H:

from contextlib import ExitStack

import concourse.mybir as mybir
from concourse.masks import make_identity

F32 = mybir.dt.float32
BF16 = mybir.dt.bfloat16
U32 = mybir.dt.uint32
U8 = mybir.dt.uint8
FP8X4 = mybir.dt.float8_e4m3fn_x4
ALU = mybir.AluOpType
ACT = mybir.ActivationFunctionType
AX = mybir.AxisListType

P = 128
B, N, D, C, H, NS = 2, 1024, 1024, 1024, 16, 10
HD = C // H
HALF = N // 2
T0, T1, T2, T3 = (0.4829629131445341, 0.8365163037378079, 0.2241438680420134, -0.1294095225512604)

PAIRS = H // 2
UNITS = 8 * PAIRS
AHEAD = 12
EARLY_PAIRS = 3
RAW_BUFS = 6
ROW = 320
GROUP = 4 * ROW
PAD = 8
SHIFTS = ((2, 0, 1), (3, 1, 0), (6, 1, 1))

FLOPS = 2 * (B * N) * D * (2 * C)


def tile_causalwaveletfieldattentionbyte_pa_kernel(tc, x, k_w, k_b, v_w, v_b, scale_gain, out):
    nc = tc.nc
    with ExitStack() as ctx:
        const = ctx.enter_context(tc.tile_pool(name="const", bufs=1))
        rawp = ctx.enter_context(tc.tile_pool(name="rawp", bufs=RAW_BUFS))
        grpp = ctx.enter_context(tc.tile_pool(name="grpp", bufs=4))
        work = ctx.enter_context(tc.tile_pool(name="work", bufs=4))
        small = ctx.enter_context(tc.tile_pool(name="small", bufs=6))
        accp = ctx.enter_context(tc.tile_pool(name="accp", bufs=4))
        psum = ctx.enter_context(tc.psum_pool(name="psum", bufs=1))
        ctx.enter_context(tc.manual_schedule())

        def bank(i):
            return psum.tile([P, 512], F32, tag="b%d" % i, name="bank%d" % i)

        ident = const.tile([P, P], F32)
        make_identity(nc, ident[:])

        sg_bf = const.tile([P, NS * H], BF16)
        nc.scalar.dma_start(out=sg_bf[:], in_=scale_gain.rearrange("j h -> (j h)").partition_broadcast(P))
        biases = grpp.tile([P, 2 * C], BF16, tag="grp", align_bytes=64)
        nc.scalar.dma_start(out=biases[:, 0:C], in_=k_b.partition_broadcast(P))
        nc.scalar.dma_start(out=biases[:, C:2 * C], in_=v_b.partition_broadcast(P))
        pair_bias = const.tile([P, 2 * C], BF16)

        g = const.tile([P, NS, H], F32)
        gmax = const.tile([P, H], F32)
        gsum = const.tile([P, H], F32)
        grec = const.tile([P, H], F32)
        gone = const.tile([P, H], F32)
        pow2 = const.tile([P, NS, H], F32)
        thr2 = const.tile([P, NS, H], F32)
        tables = (pow2, thr2)
        toep = const.tile([P, H * ROW], F32)
        scratch = out[1].rearrange("c n -> (c n)")

        def gains():
            by_head = g[:].rearrange("p j h -> p h j")
            rows = toep[:].rearrange("p (h w) -> p h w", w=ROW)
            nc.vector.memset(toep[:], 0.0)
            nc.vector.tensor_copy(out=g[:], in_=sg_bf[:].rearrange("p (j h) -> p j h", j=NS))
            nc.vector.tensor_reduce(out=gmax[:], in_=by_head, axis=AX.X, op=ALU.max)
            nc.vector.tensor_tensor(out=g[:], in0=g[:], in1=gmax[:].unsqueeze(1).to_broadcast([P, NS, H]), op=ALU.subtract)
            nc.scalar.activation(out=g[:], in_=g[:], func=ACT.Exp)
            nc.vector.tensor_reduce(out=gsum[:], in_=by_head, axis=AX.X, op=ALU.add)
            nc.vector.reciprocal(out=grec[:], in_=gsum[:])
            nc.vector.tensor_tensor(out=g[:], in0=g[:], in1=grec[:].unsqueeze(1).to_broadcast([P, NS, H]), op=ALU.mult)
            nc.vector.tensor_scalar_mul(out=pow2[:], in0=g[:], scalar1=T2)
            nc.vector.scalar_tensor_tensor(
                out=pow2[:, 1:NS, :], in0=g[:, 0:NS - 1, :], scalar=T1, in1=pow2[:, 1:NS, :], op0=ALU.mult, op1=ALU.add
            )
            nc.vector.tensor_scalar_mul(out=thr2[:], in0=g[:], scalar1=T0)
            nc.vector.tensor_reduce(out=gone[:], in_=by_head, axis=AX.X, op=ALU.add)
            nc.vector.tensor_scalar_mul(out=rows[:, :, 0:1], in0=gone[:].unsqueeze(2), scalar1=T3)
            for j in range(2, NS):
                col = 2 ** (j - 2)
                nc.vector.tensor_copy(out=rows[:, :, col:col + 1], in_=pow2[:, j, :].unsqueeze(2))
            for j in range(2, NS - 1):
                col = 3 * 2 ** (j - 2)
                nc.vector.tensor_copy(out=rows[:, :, col:col + 1], in_=thr2[:, j, :].unsqueeze(2))

        def sort_biases():
            nc.vector.tensor_copy(
                out=pair_bias[:].rearrange("p (r m c) -> p m r c", m=2, c=P),
                in_=biases[:].rearrange("p (m r c) -> p m r c", m=2, c=P),
            )

        def rows_out(queue, g0, g1):
            queue.dma_start(
                out=scratch[g0 * P * GROUP:g1 * P * GROUP].rearrange("(g a w) -> a g w", a=P, w=GROUP),
                in_=toep[:, g0 * GROUP:g1 * GROUP].rearrange("p (g w) -> p g w", w=GROUP),
            )

        def blocks_back(queue, gi):
            used = 3 * ROW + 2 * P
            skewed = scratch[gi * P * GROUP:gi * P * GROUP + P * (GROUP - 1)].rearrange("(a w) -> a w", w=GROUP - 1)
            queue.dma_start(out=toep[:, gi * GROUP:gi * GROUP + used], in_=skewed[:, 0:used])

        xq = const.tile([P, 2 * B * N], U32, align_bytes=64)
        xs = const.tile([P, 2 * B * N], U8, align_bytes=64)
        wq = const.tile([P, 2 * 2 * C], U32, align_bytes=64)
        ws = const.tile([P, 2 * 2 * C], U8, align_bytes=64)
        xq_v = xq[:].rearrange("p (g c) -> p g c", g=2)
        xs_v = xs[:].rearrange("p (g c) -> p g c", g=2)
        wq_v = wq[:].rearrange("p (g c) -> p g c", g=2)
        ws_v = ws[:].rearrange("p (g c) -> p g c", g=2)

        field = const.tile([P, 8 * H * 2 * HD], F32)
        field_v = field[:].rearrange("p (q h b c) -> p q h b c", q=8, h=H, b=2)

        raw, flipped, grouped = {}, {}, {}

        def load_slab(slab):
            kind, i = slab
            raw[slab] = rawp.tile([P, 2 * D], BF16, tag="raw", name="raw")
            halves = raw[slab][:].rearrange("p (r d) -> p r d", r=2)
            if kind == "x":
                tokens = x[i // 4, ((i // 2) % 2) * HALF:((i // 2) % 2 + 1) * HALF, :].rearrange("(a r) d -> a r d", r=4)
                nc.sync.dma_start(out=halves, in_=tokens[:, 2 * (i % 2):2 * (i % 2) + 2, :])
            else:
                nc.sync.dma_start(out=halves[:, 0, :], in_=k_w[i * P:(i + 1) * P, :])
                nc.sync.dma_start(out=halves[:, 1, :], in_=v_w[i * P:(i + 1) * P, :])

        def flip(slab, j, bk):
            words = raw[slab][:].bitcast(F32)
            flipped[slab, j] = bank(bk)
            for gu in range(4):
                nc.tensor.transpose(
                    flipped[slab, j][:, gu * P:(gu + 1) * P], words[:, j * 512 + gu * P:j * 512 + (gu + 1) * P], ident[:]
                )

        def regroup(slab, j):
            if j == 0:
                grouped[slab] = grpp.tile([P, 2 * C], BF16, tag="grp", align_bytes=64, name="grp")
            dst = grouped[slab][:].bitcast(F32).rearrange("p (g c u) -> p g c u", g=2, u=2)[:, :, j * P:(j + 1) * P, :]
            nc.scalar.copy(out=dst, in_=flipped[slab, j][:].rearrange("p (g u c) -> p g c u", g=2, u=2))

        def quantise(slab):
            kind, i = slab
            codes, scales = (xq_v, xs_v) if kind == "x" else (wq_v, ws_v)
            for gg in range(2):
                nc.vector.quantize_mx(
                    out=codes[:, gg, i * 256:(i + 1) * 256].bitcast(FP8X4),
                    scales=scales[:, gg, i * 256:(i + 1) * 256],
                    in_=grouped[slab][:, gg * C:(gg + 1) * C],
                )

        sums, biased, squares, norms = {}, {}, {}, {}

        def project(u, bk):
            if not 0 <= u < UNITS:
                return
            pr = u // 8
            sums[u] = bank(bk)
            for ti in range(2):
                t = 2 * (u % 8) + ti
                for gg in range(2):
                    nc.tensor.matmul_mx(
                        out=sums[u][:, ti * 256:(ti + 1) * 256],
                        lhsT=xq_v[:, gg, t * P:(t + 1) * P].bitcast(FP8X4),
                        lhsT_scale=xs_v[:, gg, t * P:(t + 1) * P],
                        rhs=wq_v[:, gg, pr * 256:(pr + 1) * 256].bitcast(FP8X4),
                        rhs_scale=ws_v[:, gg, pr * 256:(pr + 1) * 256],
                        start=(gg == 0),
                        stop=(gg == 1),
                    )

        def add_bias(u):
            if not 0 <= u < UNITS:
                return
            pr = u // 8
            biased[u] = work.tile([P, 512], F32, tag="kv", name="kv")
            nc.vector.tensor_tensor(
                out=biased[u][:].rearrange("p (t c) -> p t c", t=2),
                in0=sums[u][:].rearrange("p (t c) -> p t c", t=2),
                in1=pair_bias[:, pr * 256:(pr + 1) * 256].unsqueeze(1).to_broadcast([P, 2, 256]),
                op=ALU.add,
            )

        def square(u):
            if not 0 <= u < UNITS:
                return
            squares[u] = small.tile([P, 4], F32, tag="msq", name="msq")
            for th in range(4):
                lo = (th // 2) * 256 + (th % 2) * HD
                nc.scalar.activation(
                    out=biased[u][:, lo:lo + HD], in_=biased[u][:, lo:lo + HD], func=ACT.Square,
                    accum_out=squares[u][:, th:th + 1],
                )

        def root(u):
            if not 0 <= u < UNITS:
                return
            norms[u] = small.tile([P, 4], F32, tag="mag", name="mag")
            nc.scalar.activation(out=norms[u][:], in_=squares[u][:], func=ACT.Sqrt)

        def make_field(u):
            if not 0 <= u < UNITS:
                return
            pr, t = u // 8, 2 * (u % 8)
            nc.gpsimd.tensor_tensor(
                out=field_v[:, t % 8:t % 8 + 2, 2 * pr:2 * pr + 2, t // 8, :],
                in0=biased[u][:].rearrange("p (t m h c) -> p t m h c", t=2, m=2, h=2)[:, :, 1, :, :],
                in1=norms[u][:].rearrange("p (t h) -> p t h", t=2).unsqueeze(3).to_broadcast([P, 2, 2, HD]),
                op=ALU.mult,
            )

        def in_order(ap):
            return ap.rearrange("p (a r) -> p a r", r=4)

        def planes(ap):
            return ap.rearrange("p (r a) -> p a r", r=4)

        def stationary(h, q):
            return field_v[:, q, h, :, :].rearrange("p b c -> p (b c)")

        copy_f, toeplitz, acc, first_tap = {}, {}, {}, {}

        def open_head(h):
            for half in range(2):
                copy_f[h, half] = bank(2 * (h % 2) + half)
                for r in range(4):
                    nc.tensor.transpose(copy_f[h, half][:, r * P:(r + 1) * P], stationary(h, 4 * half + r), ident[:])
            for half in range(2):
                acc[h, half] = accp.tile([P, HALF + PAD], F32, tag="acc%d" % half, name="acc")
                nc.gpsimd.memset(acc[h, half][:, HALF:HALF + PAD], 0.0)

        def filter_matmul(h, i):
            near = toep[:, h * ROW:h * ROW + P]
            far = toep[:, h * ROW + P:h * ROW + 2 * P]
            if i == 0 or i == 4:
                toeplitz[h, i // 4] = bank(4 + i // 4)
            if i < 4:
                nc.tensor.matmul(toeplitz[h, 0][:, i * P:(i + 1) * P], lhsT=stationary(h, i), rhs=near, start=True, stop=True)
            else:
                r = (i - 4) // 2
                dst = toeplitz[h, 1][:, r * P:(r + 1) * P]
                if i % 2 == 0:
                    nc.tensor.matmul(dst, lhsT=stationary(h, r), rhs=far, start=True, stop=False)
                else:
                    nc.tensor.matmul(dst, lhsT=stationary(h, 4 + r), rhs=near, start=False, stop=True)

        def empty_toeplitz(h, half):
            if 0 <= h < H:
                nc.scalar.copy(out=in_order(acc[h, half][:, 0:HALF]), in_=planes(toeplitz[h, half][:]))

        def shift_one(h, half):
            if not 0 <= h < H:
                return
            if half == 0:
                first_tap[h] = accp.tile([P, N + PAD], F32, tag="one", bufs=3, name="one")
            lo = half * HALF + 1
            nc.scalar.activation(
                out=in_order(first_tap[h][:, lo:lo + HALF]), in_=planes(copy_f[h, half][:]), func=ACT.Copy,
                scale=pow2[:, 0, h:h + 1],
            )

        def tap(h, half, which):
            if not 0 <= h < H:
                return
            shift, table, j = SHIFTS[which]
            window = in_order(acc[h, half][:, shift:shift + HALF])
            nc.vector.scalar_tensor_tensor(
                out=window, in0=planes(copy_f[h, half][:]), scalar=tables[table][:, j, h:h + 1], in1=window,
                op0=ALU.mult, op1=ALU.add,
            )

        def finish(h, half):
            if not 0 <= h < H:
                return
            a0, a1, one = acc[h, 0], acc[h, 1], first_tap[h]
            if half == 0:
                nc.gpsimd.tensor_tensor(out=a0[:, 1:HALF], in0=a0[:, 1:HALF], in1=one[:, 1:HALF], op=ALU.add)
            else:
                nc.gpsimd.tensor_tensor(out=a1[:, 0:PAD], in0=a1[:, 0:PAD], in1=a0[:, HALF:HALF + PAD], op=ALU.add)
                nc.gpsimd.tensor_tensor(out=a1[:, 0:HALF], in0=a1[:, 0:HALF], in1=one[:, HALF:N], op=ALU.add)
            for b in range(2):
                nc.sync.dma_start(
                    out=out[b, h * HD:(h + 1) * HD, half * HALF:(half + 1) * HALF],
                    in_=acc[h, half][b * HD:(b + 1) * HD, 0:HALF],
                )

        slabs = [("w", 0)] + [("x", i) for i in range(8)] + [("w", pr) for pr in range(1, PAIRS)]
        early = 8 + EARLY_PAIRS
        for slab in slabs[0:RAW_BUFS]:
            load_slab(slab)
        gains()
        rows_out(nc.gpsimd, 0, 1)
        blocks_back(nc.gpsimd, 0)
        turn = 0
        for s in range(AHEAD + 4):
            if s < early:
                flip(slabs[s], 0, turn % 8)
                flip(slabs[s], 1, (turn + 1) % 8)
                turn += 2
                if s + RAW_BUFS < len(slabs):
                    load_slab(slabs[s + RAW_BUFS])
            if s >= 4:
                project(s - 4, turn % 8)
                turn += 1
            if 1 <= s <= early:
                regroup(slabs[s - 1], 0)
                regroup(slabs[s - 1], 1)
            square(s - 6)
            root(s - 7)
            make_field(s - 7)
            add_bias(s - 5)
            if 1 <= s <= early:
                quantise(slabs[s - 1])
            if s == 1:
                sort_biases()
        add_bias(AHEAD - 1)
        rows_out(nc.sync, 1, 4)
        for gi in range(1, 4):
            blocks_back(nc.sync, gi)

        def late_slab(h):
            return slabs[early + h // 2] if 0 <= h < 2 * (PAIRS - EARLY_PAIRS) else None

        def late_weights_in(h):
            if late_slab(h) is not None:
                flip(late_slab(h), h % 2, 4)

        def late_weights_out(h):
            if late_slab(h) is not None:
                regroup(late_slab(h), h % 2)

        def late_weights_quantise(h):
            if h % 2 == 1 and late_slab(h) is not None:
                quantise(late_slab(h))

        def slot(h, p):
            u = AHEAD + 4 * h + p
            if p == 0:
                empty_toeplitz(h - 1, 1)
                finish(h - 2, 1)
            project(u, 6 + u % 2)
            if u - 1 >= AHEAD:
                add_bias(u - 1)
            square(u - 2)
            root(u - 3)
            make_field(u - 3)
            if p == 0:
                tap(h - 1, 0, 1)
                tap(h - 1, 1, 0)
            elif p == 1:
                shift_one(h, 0)
                tap(h - 1, 0, 2)
                late_weights_quantise(h - 1)
            elif p == 2:
                empty_toeplitz(h, 0)
                finish(h - 1, 0)
                tap(h - 1, 1, 1)
            else:
                late_weights_out(h)
                tap(h - 1, 1, 2)
                tap(h, 0, 0)
                shift_one(h, 1)

        for h in range(H + 2):
            if h < H:
                open_head(h)
                for i in range(12):
                    filter_matmul(h, i)
                    if i == 9:
                        late_weights_in(h)
                    if i % 3 == 1:
                        slot(h, i // 3)
            else:
                for p in range(4):
                    slot(h, p)
